import numpy as np
import ml_dtypes


def mxq(x, axis, fmt="e4m3"):
    dtype, down = {"e4m3": (ml_dtypes.float8_e4m3fn, 7), "e5m2": (ml_dtypes.float8_e5m2, 14)}[fmt]
    v = np.moveaxis(np.asarray(x, np.float32).astype(ml_dtypes.bfloat16).astype(np.float64), axis, -1)
    blocks = v.reshape(v.shape[:-1] + (-1, 32))
    amax = np.abs(blocks).max(-1, keepdims=True)
    byte = np.maximum(np.where(amax > 0, np.frexp(amax)[1] - 1 + 127, 0) - down, 1)
    scale = np.exp2(byte - 127.0)
    codes = (blocks / scale).astype(np.float32).astype(dtype).astype(np.float64)
    return np.moveaxis((codes * scale).reshape(v.shape), -1, axis)


WIDE = False


def mx_kscale(k):
    if not WIDE:
        return np.ones(k)
    levels = np.array([10, -10, 5, -5, 0])
    if k % 512:
        return np.exp2(np.random.permutation(np.resize(levels, k // 32))).repeat(32)
    a = np.empty((k // 512, 16))
    for p in range(k // 512):
        a[p, :8] = np.random.permutation(np.resize(levels, 8))
        for g in range(8):
            far = levels[np.abs(levels - a[p, g]) >= 10]
            a[p, g + 8] = far[np.random.randint(len(far))]
    return np.exp2(a.ravel()).repeat(32)


BF16 = ml_dtypes.bfloat16


def bf(x):
    return np.asarray(x, np.float32).astype(BF16)


def f64(x):
    return np.asarray(x).astype(np.float64)


B, S, DV, D, H, A = 2, 256, 1024, 1024, 8, 64
LN_EPS = 1e-3


def draw0():
    s = mx_kscale(DV)
    return {
        "attn": bf(np.random.standard_normal((B, H, S, DV)) * 0.4 * s),
        "Wo": bf(np.random.standard_normal((H, DV, D)) * 0.6 / np.sqrt(DV * H) / s[None, :, None]),
        "bo": bf(np.random.standard_normal((H, D)) * 0.12 / np.sqrt(H)),
        "query_inputs": bf(np.random.standard_normal((B, S, D)) * 0.1),
        "gamma": bf(1.0 + 0.1 * np.random.standard_normal(D)),
        "beta": bf(0.1 * np.random.standard_normal(D)),
    }


def core(attn, Wo, bo, query_inputs, gamma, beta):
    pre = mxq(f64(attn), 3, "e4m3") @ mxq(f64(Wo), 1, "e4m3")
    head_out = np.maximum(pre + f64(bo)[None, :, None, :], 0.0)
    x = f64(query_inputs) + head_out.sum(axis=1)
    mean = x.mean(axis=-1, keepdims=True)
    var = x.var(axis=-1, keepdims=True)
    return f64(gamma) * (x - mean) / np.sqrt(var + LN_EPS) + f64(beta)


def e4m3fn_bytes(y):
    return np.clip(np.asarray(y, np.float64), -448.0, 448.0).astype(np.float32).astype(ml_dtypes.float8_e4m3fn).view(np.uint8)


def e4m3fn_values(b):
    return np.asarray(b, np.uint8).view(ml_dtypes.float8_e4m3fn).astype(np.float64)


def setup_inputs():
    d = draw0()
    x0 = np.asarray(d['Wo']).astype(np.float64)
    s = (np.max(np.abs(x0), axis=(0, 2), keepdims=True) / 448.0).astype(np.float32)
    out = {}
    for k, v in d.items():
        if k == 'Wo':
            out['Wo_bytes'] = e4m3fn_bytes(x0 / s.astype(np.float64))
            out['Wo_scale'] = s
        else:
            out[k] = v
    return out


def reference(attn, Wo_bytes, Wo_scale, bo, query_inputs, gamma, beta):
    return core(attn, e4m3fn_values(Wo_bytes) * Wo_scale.astype(np.float64), bo, query_inputs, gamma, beta)

@@ -1,0 +1,354 @@
+from contextlib import ExitStack
+
+import concourse.mybir as mybir
+from concourse.masks import make_identity
+
+B, H, S, DV, D = 2, 8, 256, 1024, 1024
+LN_EPS = 1e-3
+FLOPS = 2 * B * H * S * DV * D
+
+F32 = mybir.dt.float32
+BF16 = mybir.dt.bfloat16
+U32 = mybir.dt.uint32
+U8 = mybir.dt.uint8
+FP8 = mybir.dt.float8_e4m3fn
+FP8X4 = mybir.dt.float8_e4m3fn_x4
+ACT = mybir.ActivationFunctionType
+ALU = mybir.AluOpType
+AX = mybir.AxisListType
+
+P = 128
+NTOK = B * S
+NJ = NTOK // P
+HALF = 512
+NPART = 2 * H
+WA = 2
+
+V_WIDEN = {0: (1, 3, 4, 5, 7), 1: (5, 6, 7), 2: (6, 7)}
+V_WIDEN_STEADY = {0: (7,), 1: (6, 7)}
+
+
+def tile_multiheadattentionunit_pa_kernel(tc, attn, Wo_bytes, Wo_scale, bo, query_inputs, gamma, beta, out):
+    nc = tc.nc
+    with ExitStack() as ctx:
+        const = ctx.enter_context(tc.tile_pool(name="const", bufs=1))
+        wb_pool = ctx.enter_context(tc.tile_pool(name="wb", bufs=3))
+        wide_pool = ctx.enter_context(tc.tile_pool(name="wide", bufs=3))
+        grp_pool = ctx.enter_context(tc.tile_pool(name="grp", bufs=2))
+        wc_pool = ctx.enter_context(tc.tile_pool(name="wc", bufs=3))
+        at_pool = ctx.enter_context(tc.tile_pool(name="at", bufs=6))
+        ag_pool = ctx.enter_context(tc.tile_pool(name="ag", bufs=3))
+        ac_pool = ctx.enter_context(tc.tile_pool(name="ac", bufs=3))
+        r_pool = ctx.enter_context(tc.tile_pool(name="r", bufs=4))
+        ln_pool = ctx.enter_context(tc.tile_pool(name="ln", bufs=2))
+        ps_acc = ctx.enter_context(tc.psum_pool(name="ps_acc", bufs=1))
+        ps_mx = ctx.enter_context(tc.psum_pool(name="ps_mx", bufs=1))
+        ps_tr = ctx.enter_context(tc.psum_pool(name="ps_tr", bufs=2))
+        ctx.enter_context(tc.manual_schedule())
+
+        wb, wide, grp, wc, ws, at, ag, ac, asc = {}, {}, {}, {}, {}, {}, {}, {}, {}
+
+        def load_w(h):
+            wb[h] = wb_pool.tile([P, 8, D], U8, name="wbytes")
+            for g in range(2):
+                nc.sync.dma_start(
+                    out=wb[h][:, 4 * g : 4 * g + 4, :],
+                    in_=Wo_bytes[h, 512 * g : 512 * (g + 1), :].rearrange("(p t) n -> p t n", t=4),
+                )
+
+        def load_a(h):
+            for b in range(B):
+                at[h, b] = at_pool.tile([P, 2, DV], BF16, name="araw")
+                nc.sync.dma_start(out=at[h, b][:], in_=attn[b, h].rearrange("(j p) k -> p j k", p=P))
+
+        w_scale = const.tile([P, 8], F32, name="w_scale")
+        nc.sync.dma_start(
+            out=w_scale[:].rearrange("p (g t) -> p g t", g=2),
+            in_=Wo_scale.rearrange("o (g p t) x -> p (o g) (t x)", g=2, p=P, t=4),
+        )
+        bo_rows = const.tile([P, P], BF16, name="bo_rows")
+        nc.vector.memset(bo_rows[:], 0.0)
+        nc.sync.dma_start(out=bo_rows[0 : 8 * H, :], in_=bo.rearrange("h (c p) -> (h c) p", p=P))
+        load_w(0)
+        load_a(0)
+        load_w(1)
+        load_a(1)
+        q_sb = const.tile([P, NJ, D], BF16, name="q_sb")
+        nc.sync.dma_start(out=q_sb[:], in_=query_inputs.rearrange("b (j p) d -> p (b j) d", p=P))
+        load_w(2)
+        load_a(2)
+
+        ident_f = const.tile([P, P], F32, name="ident_f")
+        make_identity(nc, ident_f[:])
+        ident_b = const.tile([P, P], BF16, name="ident_b")
+        make_identity(nc, ident_b[:])
+
+        one = const.tile([P, 1], F32, name="one")
+        nc.vector.memset(one[:], 1.0)
+        one2 = const.tile([P, 1], F32, name="one2")
+        nc.scalar.activation(out=one2[:], in_=one[:], func=ACT.Sqrt)
+
+        bcol = const.tile([P, 8 * H], F32, name="bcol")
+        negb = const.tile([P, 8 * H], F32, name="negb")
+        btot = const.tile([P, 8], F32, name="btot")
+        acc_t = const.tile([P, 4, NTOK], F32, name="acc_t")
+        gam = const.tile([P, D], BF16, name="gam")
+        bet = const.tile([P, D], BF16, name="bet")
+        acc_a = [ps_acc.tile([P, HALF], F32, name="acc_a%d" % j) for j in range(NJ)]
+
+        def prepare_bias():
+            bo_t = ps_tr.tile([P, P], BF16, name="bo_t", tag="tr")
+            nc.tensor.transpose(bo_t[:], bo_rows[:], ident_b[:])
+            nc.vector.tensor_copy(out=bcol[:], in_=bo_t[:, 0 : 8 * H])
+            nc.vector.tensor_scalar(out=negb[:], in0=bcol[:], scalar1=-1.0, scalar2=None, op0=ALU.mult)
+            nc.vector.tensor_reduce(out=btot[:], in_=bcol[:].rearrange("p (h c) -> p c h", h=H), axis=AX.X, op=ALU.add)
+
+        def open_acc():
+            for j in range(NJ):
+                nc.tensor.matmul(out=acc_a[j][:], lhsT=ident_b[:], rhs=q_sb[:, j, 0:HALF], start=True, stop=False)
+
+        def widen(k, gt, eng):
+            h, s = divmod(k, 2)
+            c0 = HALF if s == 0 else 0
+            src = wb[h][:, gt, c0 : c0 + HALF].bitcast(FP8)
+            if eng == "v":
+                nc.vector.tensor_scalar(out=wide[k][:, gt, :], in0=src, scalar1=w_scale[:, gt : gt + 1], scalar2=None, op0=ALU.mult)
+            else:
+                nc.scalar.activation(out=wide[k][:, gt, :], in_=src, func=ACT.Copy, scale=w_scale[:, gt : gt + 1])
+
+        def interleave(k):
+            grp[k] = grp_pool.tile([P, 8 * HALF], BF16, name="grp", align_bytes=64)
+            nc.vector.tensor_copy(
+                out=grp[k][:].rearrange("p (g n t) -> p g n t", g=2, t=4),
+                in_=wide[k][:].rearrange("p (g t) n -> p g n t", g=2),
+            )
+
+        def quant_w(k):
+            wc[k] = wc_pool.tile([P, 2 * HALF], U32, name="wcodes", align_bytes=64)
+            ws[k] = wc_pool.tile([P, 2 * HALF], U8, name="wscales", align_bytes=64)
+            nc.vector.quantize_mx(out=wc[k][:].bitcast(FP8X4), scales=ws[k][:], in_=grp[k][:])
+
+        xt = {}
+
+        def a_transpose(a, b):
+            h, g = divmod(a, 2)
+            xt[a, b] = ps_tr.tile([P, 2, 2 * P], F32, name="xt", tag="tr")
+            for j in range(2):
+                words = at[h, b][:, j, :].bitcast(F32)
+                for u in range(2):
+                    nc.tensor.transpose(xt[a, b][:, u, P * j : P * (j + 1)], words[:, 256 * g + u : 256 * (g + 1) : 2], ident_f[:])
+
+        def a_evac(a, b):
+            if b == 0:
+                ag[a] = ag_pool.tile([P, 4 * NTOK], BF16, name="agrp", align_bytes=64)
+            nc.scalar.copy(
+                out=ag[a][:, 1024 * b : 1024 * (b + 1)].bitcast(F32).rearrange("p (r u) -> p r u", u=2),
+                in_=xt[a, b][:].rearrange("p u r -> p r u"),
+            )
+
+        def quant_a(a):
+            h, g = divmod(a, 2)
+            if g == 0:
+                ac[h] = ac_pool.tile([P, 2, NTOK], U32, name="acodes", align_bytes=64)
+                asc[h] = ac_pool.tile([P, 2, NTOK], U8, name="ascales", align_bytes=64)
+            nc.vector.quantize_mx(out=ac[h][:, g, :].bitcast(FP8X4), scales=asc[h][:, g, :], in_=ag[a][:])
+
+        mx = {}
+        r = {}
+
+        def product(k, cc, pool, tag):
+            h = k // 2
+            mx[k, cc] = pool.tile([P, NTOK], F32, name="mx", tag=tag)
+            for g in range(2):
+                cols = slice(HALF * g + P * cc, HALF * g + P * (cc + 1))
+                nc.tensor.matmul_mx(
+                    out=mx[k, cc][:],
+                    lhsT=wc[k][:, cols].bitcast(FP8X4),
+                    lhsT_scale=ws[k][:, cols],
+                    rhs=ac[h][:, g, :].bitcast(FP8X4),
+                    rhs_scale=asc[h][:, g, :],
+                    start=(g == 0),
+                    stop=(g == 1),
+                )
+
+        def empty(k, cc, eng="s"):
+            h, s = divmod(k, 2)
+            if s == 0:
+                col = 8 * h + 4 + cc
+                if h == 0:
+                    nc.vector.tensor_scalar(out=acc_t[:, cc, :], in0=mx[k, cc][:], scalar1=negb[:, col : col + 1],
+                                            scalar2=btot[:, 4 + cc : 5 + cc], op0=ALU.max, op1=ALU.add)
+                else:
+                    nc.vector.scalar_tensor_tensor(out=acc_t[:, cc, :], in0=mx[k, cc][:], scalar=negb[:, col : col + 1],
+                                                   in1=acc_t[:, cc, :], op0=ALU.max, op1=ALU.add)
+            else:
+                col = 8 * h + cc
+                r[k, cc] = r_pool.tile([P, NTOK], F32, name="relu")
+                if eng == "s":
+                    nc.scalar.activation(out=r[k, cc][:], in_=mx[k, cc][:], func=ACT.Relu, bias=bcol[:, col : col + 1])
+                else:
+                    nc.vector.tensor_scalar(out=r[k, cc][:], in0=mx[k, cc][:], scalar1=bcol[:, col : col + 1], scalar2=0.0,
+                                            op0=ALU.add, op1=ALU.max)
+
+        def add_up(k, cc):
+            last = k == NPART - 1 and cc == 3
+            for j in range(NJ):
+                nc.tensor.matmul(out=acc_a[j][:, P * cc : P * (cc + 1)], lhsT=r[k, cc][:, P * j : P * (j + 1)], rhs=ident_f[:],
+                                 is_transpose=True, start=False, stop=last)
+
+        def groups(k):
+            pb = 2 * ((k - 1) // 2)
+            cb = (0, 1) if k % 2 == 1 else (2, 3)
+            pa = k - 1 if k % 2 == 0 else k - 2
+            ca = (0, 1) if k % 2 == 0 else (2, 3)
+            gb = [(pb, cc) for cc in cb] if 0 <= pb < NPART and k >= 1 else []
+            ga = [(pa, cc) for cc in ca] if 1 <= pa < NPART - 1 else []
+            return gb, ga
+
+        pending = []
+
+        def tick(k):
+            a, qa, kw = k + 2, k + 1, k + WA
+            has_a = 0 <= a < NPART
+            has_q = 0 <= qa < NPART
+            has_w = 0 <= kw < NPART
+            has_k = 0 <= k < NPART
+            gb, ga = groups(k)
+            gb_next, ga_next = groups(k + 1)
+            s_list = []
+            v_list = []
+            if has_w:
+                wide[kw] = wide_pool.tile([P, 8, HALF], BF16, name="wide")
+                v_list = list(V_WIDEN.get(kw, V_WIDEN_STEADY[kw % 2]))
+                s_list = [gt for gt in range(8) if gt not in v_list]
+
+            def s_widen(n):
+                for gt in s_list[0:n]:
+                    widen(kw, gt, "s")
+                    s_list.remove(gt)
+
+            def v_widen(n):
+                for gt in v_list[0:n]:
+                    widen(kw, gt, "v")
+                    v_list.remove(gt)
+
+            if ga:
+                empty(*ga[0])
+            if has_a:
+                a_transpose(a, 0)
+            for item in pending:
+                add_up(*item)
+            pending.clear()
+            if ga:
+                product(ga[1][0], ga[1][1], ps_mx, "mxa")
+            if has_k:
+                interleave(k)
+            else:
+                v_widen(8)
+            s_widen(2)
+            if k < 0:
+                s_widen(8)
+            if has_a:
+                a_evac(a, 0)
+            if ga:
+                empty(*ga[1])
+                pending.append(ga[1])
+            if has_a:
+                a_transpose(a, 1)
+            if ga:
+                add_up(*ga[0])
+            if gb:
+                empty(*gb[0])
+                product(gb[1][0], gb[1][1], ps_mx, "mxb")
+            s_widen(2)
+            if k == 0:
+                quant_a(0)
+            if has_k:
+                quant_w(k)
+            if has_q and qa > 0:
+                quant_a(qa)
+            if ga_next:
+                product(ga_next[0][0], ga_next[0][1], ps_mx, "mxa")
+            if has_a:
+                a_evac(a, 1)
+            if gb:
+                empty(*gb[1])
+            if gb_next:
+                product(gb_next[0][0], gb_next[0][1], ps_mx, "mxb")
+            s_widen(8)
+            v_widen(8)
+            if k >= 0 and k % 2 == 0 and k // 2 + 3 < H:
+                load_w(k // 2 + 3)
+                load_a(k // 2 + 3)
+            if k == 8:
+                nc.sync.dma_start(out=gam[:], in_=gamma.partition_broadcast(P))
+                nc.sync.dma_start(out=bet[:], in_=beta.partition_broadcast(P))
+
+        prepare_bias()
+        tick(-2)
+        tick(-1)
+        tick(0)
+        open_acc()
+        for k in range(1, NPART + 1):
+            tick(k)
+        for item in pending:
+            add_up(*item)
+
+        acc_b = {}
+
+        def turn_b(j, pool, tag):
+            acc_b[j] = pool.tile([P, HALF], F32, name="acc_b", tag=tag)
+            nc.tensor.matmul(out=acc_b[j][:], lhsT=ident_b[:], rhs=q_sb[:, j, HALF:D], start=True, stop=False)
+            for cc in range(4):
+                nc.tensor.matmul(out=acc_b[j][:, P * cc : P * (cc + 1)], lhsT=acc_t[:, cc, P * j : P * (j + 1)], rhs=ident_f[:],
+                                 is_transpose=True, start=False, stop=(cc == 3))
+
+        kl = NPART - 1
+        product(kl, 0, ps_mx, "mxa")
+        product(kl, 1, ps_mx, "mxb")
+        product(kl, 2, ps_tr, "tr")
+        product(kl, 3, ps_tr, "tr")
+        empty(kl, 0, "s")
+        empty(kl, 1, "v")
+        empty(kl, 2, "s")
+        empty(kl, 3, "v")
+        add_up(kl, 0)
+        turn_b(0, ps_mx, "mxa")
+        add_up(kl, 1)
+        turn_b(1, ps_mx, "mxb")
+        add_up(kl, 2)
+        turn_b(2, ps_tr, "tr")
+        add_up(kl, 3)
+        turn_b(3, ps_tr, "tr")
+
+        out_rows = out.rearrange("b (j p) d -> (b j) p d", p=P)
+        stats = const.tile([P, NJ, 2, 6], F32, name="stats")
+        mv = const.tile([P, NJ, 2], F32, name="mv")
+        rstd = const.tile([P, NJ], F32, name="rstd")
+
+        def ln_stats(j):
+            nc.vector.bn_stats(out=stats[:, j, 1, :], in_=acc_b[j][:])
+            nc.vector.bn_stats(out=stats[:, j, 0, :], in_=acc_a[j][:])
+            nc.vector.bn_aggr(out=mv[:, j, :], in_=stats[:, j, :, :].rearrange("p a b -> p (a b)"))
+            nc.vector.tensor_scalar(out=rstd[:, j : j + 1], in0=mv[:, j, 1:2], scalar1=LN_EPS, scalar2=None, op0=ALU.add)
+            nc.scalar.activation(out=rstd[:, j : j + 1], in_=rstd[:, j : j + 1], func=ACT.Sqrt)
+
+        def ln_apply(j):
+            nc.vector.reciprocal(out=rstd[:, j : j + 1], in_=rstd[:, j : j + 1])
+            cen = ln_pool.tile([P, D], F32, name="cen")
+            nc.vector.scalar_tensor_tensor(out=cen[:, 0:HALF], in0=acc_a[j][:], scalar=mv[:, j, 0:1], in1=gam[:, 0:HALF],
+                                           op0=ALU.subtract, op1=ALU.mult)
+            nc.vector.scalar_tensor_tensor(out=cen[:, HALF:D], in0=acc_b[j][:], scalar=mv[:, j, 0:1], in1=gam[:, HALF:D],
+                                           op0=ALU.subtract, op1=ALU.mult)
+            res = ln_pool.tile([P, D], F32, name="res")
+            nc.vector.scalar_tensor_tensor(out=res[:], in0=cen[:], scalar=rstd[:, j : j + 1], in1=bet[:], op0=ALU.mult, op1=ALU.add)
+            nc.sync.dma_start(out=out_rows[j], in_=res[:])
+
+        ln_stats(0)
+        ln_stats(1)
+        ln_apply(0)
+        ln_stats(2)
+        ln_apply(1)
+        ln_stats(3)
+        ln_apply(2)
+        ln_apply(3)

@@ -22,9 +22,9 @@ NTOK = B * S
 NJ = NTOK // P
 HALF = 512
 NPART = 2 * H
-WA = 2
+WA = 3
 
-V_WIDEN = {0: (1, 3, 4, 5, 7), 1: (5, 6, 7), 2: (6, 7)}
+V_WIDEN = {0: (1, 3, 4, 5, 7), 1: (4, 5, 6, 7), 2: (5, 6, 7), 3: (6, 7)}
 V_WIDEN_STEADY = {0: (7,), 1: (6, 7)}
 
 
@@ -33,7 +33,7 @@ def tile_multiheadattentionunit_pa_kernel(tc, attn, Wo_bytes, Wo_scale, bo, quer
     with ExitStack() as ctx:
         const = ctx.enter_context(tc.tile_pool(name="const", bufs=1))
         wb_pool = ctx.enter_context(tc.tile_pool(name="wb", bufs=3))
-        wide_pool = ctx.enter_context(tc.tile_pool(name="wide", bufs=3))
+        wide_pool = ctx.enter_context(tc.tile_pool(name="wide", bufs=4))
         grp_pool = ctx.enter_context(tc.tile_pool(name="grp", bufs=2))
         wc_pool = ctx.enter_context(tc.tile_pool(name="wc", bufs=3))
         at_pool = ctx.enter_context(tc.tile_pool(name="at", bufs=6))
@@ -70,12 +70,12 @@ def tile_multiheadattentionunit_pa_kernel(tc, attn, Wo_bytes, Wo_scale, bo, quer
         nc.vector.memset(bo_rows[:], 0.0)
         nc.sync.dma_start(out=bo_rows[0 : 8 * H, :], in_=bo.rearrange("h (c p) -> (h c) p", p=P))
         load_w(0)
-        load_a(0)
         load_w(1)
+        load_a(0)
         load_a(1)
+        load_w(2)
         q_sb = const.tile([P, NJ, D], BF16, name="q_sb")
         nc.sync.dma_start(out=q_sb[:], in_=query_inputs.rearrange("b (j p) d -> p (b j) d", p=P))
-        load_w(2)
         load_a(2)
 
         ident_f = const.tile([P, P], F32, name="ident_f")
@@ -117,11 +117,18 @@ def tile_multiheadattentionunit_pa_kernel(tc, attn, Wo_bytes, Wo_scale, bo, quer
                 nc.scalar.activation(out=wide[k][:, gt, :], in_=src, func=ACT.Copy, scale=w_scale[:, gt : gt + 1])
 
         def interleave(k):
-            grp[k] = grp_pool.tile([P, 8 * HALF], BF16, name="grp", align_bytes=64)
-            nc.vector.tensor_copy(
-                out=grp[k][:].rearrange("p (g n t) -> p g n t", g=2, t=4),
-                in_=wide[k][:].rearrange("p (g t) n -> p g n t", g=2),
-            )
+            interleave_pass(k, 0, "v")
+            interleave_pass(k, 1, "v")
+
+        def interleave_pass(k, g, eng):
+            if g == 0:
+                grp[k] = grp_pool.tile([P, 8 * HALF], BF16, name="grp", align_bytes=64)
+            dst = grp[k][:, 4 * HALF * g : 4 * HALF * (g + 1)].rearrange("p (c i t) -> p c t i", i=4, t=4)
+            src = wide[k][:, 4 * g : 4 * g + 4, :].rearrange("p t (c i) -> p c t i", i=4)
+            if eng == "v":
+                nc.vector.tensor_copy(out=dst, in_=src)
+            else:
+                nc.scalar.copy(out=dst, in_=src)
 
         def quant_w(k):
             wc[k] = wc_pool.tile([P, 2 * HALF], U32, name="wcodes", align_bytes=64)
@@ -261,10 +268,12 @@ def tile_multiheadattentionunit_pa_kernel(tc, attn, Wo_bytes, Wo_scale, bo, quer
                 empty(*gb[0])
                 product(gb[1][0], gb[1][1], ps_mx, "mxb")
             s_widen(2)
-            if k == 0:
-                quant_a(0)
             if has_k:
                 quant_w(k)
+            if k == 0:
+                for gt in V_WIDEN[2]:
+                    widen(2, gt, "v")
+                quant_a(0)
             if has_q and qa > 0:
                 quant_a(qa)
             if ga_next:
@@ -285,14 +294,23 @@ def tile_multiheadattentionunit_pa_kernel(tc, attn, Wo_bytes, Wo_scale, bo, quer
                 nc.sync.dma_start(out=bet[:], in_=beta.partition_broadcast(P))
 
         prepare_bias()
-        tick(-2)
-        tick(-1)
+        for kw in range(WA):
+            wide[kw] = wide_pool.tile([P, 8, HALF], BF16, name="wide")
+            for gt in range(8):
+                if gt not in V_WIDEN[kw]:
+                    widen(kw, gt, "s")
+            if kw < 2:
+                for gt in V_WIDEN[kw]:
+                    widen(kw, gt, "v")
+        for a in range(2):
+            a_transpose(a, 0)
+            a_transpose(a, 1)
+            a_evac(a, 0)
+            a_evac(a, 1)
         tick(0)
         open_acc()
-        for k in range(1, NPART + 1):
+        for k in range(1, NPART - 3):
             tick(k)
-        for item in pending:
-            add_up(*item)
 
         acc_b = {}
 
@@ -303,23 +321,71 @@ def tile_multiheadattentionunit_pa_kernel(tc, attn, Wo_bytes, Wo_scale, bo, quer
                 nc.tensor.matmul(out=acc_b[j][:, P * cc : P * (cc + 1)], lhsT=acc_t[:, cc, P * j : P * (j + 1)], rhs=ident_f[:],
                                  is_transpose=True, start=False, stop=(cc == 3))
 
-        kl = NPART - 1
-        product(kl, 0, ps_mx, "mxa")
-        product(kl, 1, ps_mx, "mxb")
-        product(kl, 2, ps_tr, "tr")
-        product(kl, 3, ps_tr, "tr")
-        empty(kl, 0, "s")
-        empty(kl, 1, "v")
-        empty(kl, 2, "s")
-        empty(kl, 3, "v")
-        add_up(kl, 0)
-        turn_b(0, ps_mx, "mxa")
-        add_up(kl, 1)
-        turn_b(1, ps_mx, "mxb")
-        add_up(kl, 2)
+        empty(11, 2)
+        a_transpose(15, 0)
+        for item in pending:
+            add_up(*item)
+        product(11, 3, ps_mx, "mxa")
+        interleave_pass(13, 0, "v")
+        interleave_pass(13, 1, "s")
+        a_evac(15, 0)
+        empty(11, 3)
+        a_transpose(15, 1)
+        add_up(11, 2)
+        add_up(11, 3)
+        empty(12, 0)
+        product(12, 1, ps_mx, "mxb")
+        interleave_pass(14, 0, "v")
+        interleave_pass(14, 1, "s")
+        quant_w(13)
+        quant_a(14)
+        product(13, 0, ps_mx, "mxa")
+        a_evac(15, 1)
+        empty(12, 1)
+        product(12, 2, ps_mx, "mxb")
+        product(12, 3, ps_tr, "tr")
+        empty(13, 0)
+        product(13, 1, ps_mx, "mxa")
+        add_up(13, 0)
+        interleave_pass(15, 0, "v")
+        interleave_pass(15, 1, "s")
+        quant_w(14)
+        quant_a(15)
+        empty(12, 2)
+        empty(12, 3)
+        product(13, 2, ps_tr, "tr")
+        product(13, 3, ps_mx, "mxb")
+        empty(13, 1)
+        empty(13, 2)
+        empty(13, 3)
+        product(14, 0, ps_tr, "tr")
+        product(14, 1, ps_mx, "mxa")
+        product(14, 2, ps_tr, "tr")
+        product(14, 3, ps_mx, "mxb")
+        add_up(13, 1)
+        add_up(13, 2)
+        add_up(13, 3)
+        empty(14, 0)
+        empty(14, 1)
+        quant_w(15)
+        product(15, 0, ps_tr, "tr")
+        product(15, 1, ps_mx, "mxa")
+        empty(14, 2)
+        empty(14, 3)
+        product(15, 2, ps_tr, "tr")
+        product(15, 3, ps_mx, "mxb")
+        empty(15, 0, "s")
+        empty(15, 1, "v")
+        empty(15, 2, "s")
+        empty(15, 3, "v")
+        add_up(15, 0)
+        add_up(15, 1)
+        add_up(15, 2)
+        add_up(15, 3)
+        turn_b(0, ps_tr, "tr")
+        turn_b(1, ps_mx, "mxa")
         turn_b(2, ps_tr, "tr")
-        add_up(kl, 3)
-        turn_b(3, ps_tr, "tr")
+        turn_b(3, ps_mx, "mxb")
 
         out_rows = out.rearrange("b (j p) d -> (b j) p d", p=P)
         stats = const.tile([P, NJ, 2, 6], F32, name="stats")
@@ -328,7 +394,6 @@ def tile_multiheadattentionunit_pa_kernel(tc, attn, Wo_bytes, Wo_scale, bo, quer
 
         def ln_stats(j):
             nc.vector.bn_stats(out=stats[:, j, 1, :], in_=acc_b[j][:])
-            nc.vector.bn_stats(out=stats[:, j, 0, :], in_=acc_a[j][:])
             nc.vector.bn_aggr(out=mv[:, j, :], in_=stats[:, j, :, :].rearrange("p a b -> p (a b)"))
             nc.vector.tensor_scalar(out=rstd[:, j : j + 1], in0=mv[:, j, 1:2], scalar1=LN_EPS, scalar2=None, op0=ALU.add)
             nc.scalar.activation(out=rstd[:, j : j + 1], in_=rstd[:, j : j + 1], func=ACT.Sqrt)
@@ -341,9 +406,17 @@ def tile_multiheadattentionunit_pa_kernel(tc, attn, Wo_bytes, Wo_scale, bo, quer
             nc.vector.scalar_tensor_tensor(out=cen[:, HALF:D], in0=acc_b[j][:], scalar=mv[:, j, 0:1], in1=gam[:, HALF:D],
                                            op0=ALU.subtract, op1=ALU.mult)
             res = ln_pool.tile([P, D], F32, name="res")
-            nc.vector.scalar_tensor_tensor(out=res[:], in0=cen[:], scalar=rstd[:, j : j + 1], in1=bet[:], op0=ALU.mult, op1=ALU.add)
-            nc.sync.dma_start(out=out_rows[j], in_=res[:])
+            if j < NJ - 1:
+                nc.vector.scalar_tensor_tensor(out=res[:], in0=cen[:], scalar=rstd[:, j : j + 1], in1=bet[:], op0=ALU.mult, op1=ALU.add)
+                nc.sync.dma_start(out=out_rows[j], in_=res[:])
+            else:
+                for c0 in (0, HALF):
+                    nc.vector.scalar_tensor_tensor(out=res[:, c0 : c0 + HALF], in0=cen[:, c0 : c0 + HALF], scalar=rstd[:, j : j + 1],
+                                                   in1=bet[:, c0 : c0 + HALF], op0=ALU.mult, op1=ALU.add)
+                    nc.sync.dma_start(out=out_rows[j][:, c0 : c0 + HALF], in_=res[:, c0 : c0 + HALF])
 
+        for j in range(NJ):
+            nc.vector.bn_stats(out=stats[:, j, 0, :], in_=acc_a[j][:])
         ln_stats(0)
         ln_stats(1)
         ln_apply(0)

@@ -22,10 +22,11 @@ NTOK = B * S
 NJ = NTOK // P
 HALF = 512
 NPART = 2 * H
+GCH = 256
 WA = 3
 
 V_WIDEN = {0: (1, 3, 4, 5, 7), 1: (4, 5, 6, 7), 2: (5, 6, 7), 3: (6, 7)}
-V_WIDEN_STEADY = {0: (7,), 1: (6, 7)}
+V_WIDEN_STEADY = {0: (6, 7), 1: (6, 7)}
 
 
 def tile_multiheadattentionunit_pa_kernel(tc, attn, Wo_bytes, Wo_scale, bo, query_inputs, gamma, beta, out):
@@ -40,7 +41,7 @@ def tile_multiheadattentionunit_pa_kernel(tc, attn, Wo_bytes, Wo_scale, bo, quer
         ag_pool = ctx.enter_context(tc.tile_pool(name="ag", bufs=3))
         ac_pool = ctx.enter_context(tc.tile_pool(name="ac", bufs=3))
         r_pool = ctx.enter_context(tc.tile_pool(name="r", bufs=4))
-        ln_pool = ctx.enter_context(tc.tile_pool(name="ln", bufs=2))
+        ln_pool = ctx.enter_context(tc.tile_pool(name="ln", bufs=3))
         ps_acc = ctx.enter_context(tc.psum_pool(name="ps_acc", bufs=1))
         ps_mx = ctx.enter_context(tc.psum_pool(name="ps_mx", bufs=1))
         ps_tr = ctx.enter_context(tc.psum_pool(name="ps_tr", bufs=2))
@@ -50,11 +51,13 @@ def tile_multiheadattentionunit_pa_kernel(tc, attn, Wo_bytes, Wo_scale, bo, quer
 
         def load_w(h):
             wb[h] = wb_pool.tile([P, 8, D], U8, name="wbytes")
-            for g in range(2):
-                nc.sync.dma_start(
-                    out=wb[h][:, 4 * g : 4 * g + 4, :],
-                    in_=Wo_bytes[h, 512 * g : 512 * (g + 1), :].rearrange("(p t) n -> p t n", t=4),
-                )
+            col_ranges = ((HALF, D), (0, HALF)) if h == 0 else ((0, D),)
+            for c0, c1 in col_ranges:
+                for g in range(2):
+                    nc.sync.dma_start(
+                        out=wb[h][:, 4 * g : 4 * g + 4, c0:c1],
+                        in_=Wo_bytes[h, 512 * g : 512 * (g + 1), c0:c1].rearrange("(p t) n -> p t n", t=4),
+                    )
 
         def load_a(h):
             for b in range(B):
@@ -70,8 +73,8 @@ def tile_multiheadattentionunit_pa_kernel(tc, attn, Wo_bytes, Wo_scale, bo, quer
         nc.vector.memset(bo_rows[:], 0.0)
         nc.sync.dma_start(out=bo_rows[0 : 8 * H, :], in_=bo.rearrange("h (c p) -> (h c) p", p=P))
         load_w(0)
-        load_w(1)
         load_a(0)
+        load_w(1)
         load_a(1)
         load_w(2)
         q_sb = const.tile([P, NJ, D], BF16, name="q_sb")
@@ -87,6 +90,9 @@ def tile_multiheadattentionunit_pa_kernel(tc, attn, Wo_bytes, Wo_scale, bo, quer
         nc.vector.memset(one[:], 1.0)
         one2 = const.tile([P, 1], F32, name="one2")
         nc.scalar.activation(out=one2[:], in_=one[:], func=ACT.Sqrt)
+
+        minus_half = const.tile([P, 1], F32, name="minus_half")
+        nc.gpsimd.memset(minus_half[:], -0.5)
 
         bcol = const.tile([P, 8 * H], F32, name="bcol")
         negb = const.tile([P, 8 * H], F32, name="negb")
@@ -302,14 +308,16 @@ def tile_multiheadattentionunit_pa_kernel(tc, attn, Wo_bytes, Wo_scale, bo, quer
             if kw < 2:
                 for gt in V_WIDEN[kw]:
                     widen(kw, gt, "v")
-        for a in range(2):
-            a_transpose(a, 0)
-            a_transpose(a, 1)
-            a_evac(a, 0)
-            a_evac(a, 1)
+            if kw == 1:
+                for a in range(2):
+                    a_transpose(a, 0)
+                    a_transpose(a, 1)
+                    a_evac(a, 0)
+                    a_evac(a, 1)
         tick(0)
+        tick(1)
         open_acc()
-        for k in range(1, NPART - 3):
+        for k in range(2, NPART - 3):
             tick(k)
 
         acc_b = {}
@@ -391,20 +399,25 @@ def tile_multiheadattentionunit_pa_kernel(tc, attn, Wo_bytes, Wo_scale, bo, quer
         stats = const.tile([P, NJ, 2, 6], F32, name="stats")
         mv = const.tile([P, NJ, 2], F32, name="mv")
         rstd = const.tile([P, NJ], F32, name="rstd")
+        s_sum = const.tile([P, 4], F32, name="s_sum")
+        g_val = const.tile([P, 8], F32, name="g_val")
+        junk = const.tile([P, HALF], F32, name="junk")
+        halves = ((acc_a, 0), (acc_b, HALF))
 
         def ln_stats(j):
             nc.vector.bn_stats(out=stats[:, j, 1, :], in_=acc_b[j][:])
             nc.vector.bn_aggr(out=mv[:, j, :], in_=stats[:, j, :, :].rearrange("p a b -> p (a b)"))
             nc.vector.tensor_scalar(out=rstd[:, j : j + 1], in0=mv[:, j, 1:2], scalar1=LN_EPS, scalar2=None, op0=ALU.add)
+
+        def ln_sqrt(j):
             nc.scalar.activation(out=rstd[:, j : j + 1], in_=rstd[:, j : j + 1], func=ACT.Sqrt)
 
         def ln_apply(j):
             nc.vector.reciprocal(out=rstd[:, j : j + 1], in_=rstd[:, j : j + 1])
             cen = ln_pool.tile([P, D], F32, name="cen")
-            nc.vector.scalar_tensor_tensor(out=cen[:, 0:HALF], in0=acc_a[j][:], scalar=mv[:, j, 0:1], in1=gam[:, 0:HALF],
-                                           op0=ALU.subtract, op1=ALU.mult)
-            nc.vector.scalar_tensor_tensor(out=cen[:, HALF:D], in0=acc_b[j][:], scalar=mv[:, j, 0:1], in1=gam[:, HALF:D],
-                                           op0=ALU.subtract, op1=ALU.mult)
+            for acc, c0 in halves:
+                nc.vector.scalar_tensor_tensor(out=cen[:, c0 : c0 + HALF], in0=acc[j][:], scalar=mv[:, j, 0:1], in1=gam[:, c0 : c0 + HALF],
+                                               op0=ALU.subtract, op1=ALU.mult)
             res = ln_pool.tile([P, D], F32, name="res")
             if j < NJ - 1:
                 nc.vector.scalar_tensor_tensor(out=res[:], in0=cen[:], scalar=rstd[:, j : j + 1], in1=bet[:], op0=ALU.mult, op1=ALU.add)
@@ -415,13 +428,35 @@ def tile_multiheadattentionunit_pa_kernel(tc, attn, Wo_bytes, Wo_scale, bo, quer
                                                    in1=bet[:, c0 : c0 + HALF], op0=ALU.mult, op1=ALU.add)
                     nc.sync.dma_start(out=out_rows[j][:, c0 : c0 + HALF], in_=res[:, c0 : c0 + HALF])
 
-        for j in range(NJ):
+        for i in range(2):
+            nc.scalar.activation(out=junk[:], in_=halves[i][0][0][:], func=ACT.Identity, accum_out=s_sum[:, i : i + 1])
+        nc.gpsimd.tensor_tensor(out=g_val[:, 0:1], in0=s_sum[:, 0:1], in1=s_sum[:, 1:2], op=ALU.add)
+        nc.gpsimd.tensor_scalar(out=g_val[:, 1:2], in0=g_val[:, 0:1], scalar1=-1.0 / D, scalar2=0.0, op0=ALU.mult, op1=ALU.add)
+        for i in range(2):
+            nc.scalar.activation(out=junk[:], in_=halves[i][0][0][:], func=ACT.Square, bias=g_val[:, 1:2], accum_out=s_sum[:, 2 + i : 3 + i])
+        nc.gpsimd.tensor_tensor(out=g_val[:, 2:3], in0=s_sum[:, 2:3], in1=s_sum[:, 3:4], op=ALU.add)
+        nc.gpsimd.tensor_scalar(out=g_val[:, 3:4], in0=g_val[:, 2:3], scalar1=1.0 / D, scalar2=LN_EPS, op0=ALU.mult, op1=ALU.add)
+        nc.gpsimd.tensor_tensor(out=g_val[:, 4:5], in0=g_val[:, 3:4], in1=minus_half[:], op=ALU.pow)
+        nc.gpsimd.tensor_tensor(out=g_val[:, 5:6], in0=g_val[:, 1:2], in1=g_val[:, 4:5], op=ALU.mult)
+
+        for j in range(1, NJ):
             nc.vector.bn_stats(out=stats[:, j, 0, :], in_=acc_a[j][:])
-        ln_stats(0)
         ln_stats(1)
-        ln_apply(0)
+        ln_sqrt(1)
         ln_stats(2)
+        ln_sqrt(2)
+        norm0 = const.tile([P, D], F32, name="norm0")
+        res0 = const.tile([P, D], F32, name="res0")
+        for acc, c0 in halves:
+            nc.scalar.activation(out=norm0[:, c0 : c0 + HALF], in_=acc[0][:], func=ACT.Identity, scale=g_val[:, 4:5], bias=g_val[:, 5:6])
+        for c0 in range(0, D, GCH):
+            cols = slice(c0, c0 + GCH)
+            nc.gpsimd.tensor_tensor(out=norm0[:, cols], in0=norm0[:, cols], in1=gam[:, cols], op=ALU.mult)
+            nc.gpsimd.tensor_tensor(out=res0[:, cols], in0=norm0[:, cols], in1=bet[:, cols], op=ALU.add)
         ln_apply(1)
         ln_stats(3)
+        ln_sqrt(3)
+        for c0 in (0, HALF):
+            nc.scalar.dma_start(out=out_rows[0][:, c0 : c0 + HALF], in_=res0[:, c0 : c0 + HALF])
         ln_apply(2)
         ln_apply(3)

@@ -26,7 +26,7 @@ GCH = 256
 WA = 3
 
 V_WIDEN = {0: (1, 3, 4, 5, 7), 1: (4, 5, 6, 7), 2: (5, 6, 7), 3: (6, 7)}
-V_WIDEN_STEADY = {0: (6, 7), 1: (6, 7)}
+V_WIDEN_STEADY = {0: (7,), 1: (6, 7)}
 
 
 def tile_multiheadattentionunit_pa_kernel(tc, attn, Wo_bytes, Wo_scale, bo, query_inputs, gamma, beta, out):

@@ -22,11 +22,10 @@ NTOK = B * S
 NJ = NTOK // P
 HALF = 512
 NPART = 2 * H
-GCH = 256
 WA = 3
 
-V_WIDEN = {0: (1, 3, 4, 5, 7), 1: (4, 5, 6, 7), 2: (5, 6, 7), 3: (6, 7)}
-V_WIDEN_STEADY = {0: (7,), 1: (6, 7)}
+V_WIDEN = {0: (1, 3, 4, 5, 7), 1: (3, 4, 5, 6, 7), 2: (4, 5, 6, 7), 3: (4, 5, 6, 7), 4: (5, 6, 7), 5: (5, 6, 7)}
+V_WIDEN_STEADY = {0: (6, 7), 1: (6, 7)}
 
 
 def tile_multiheadattentionunit_pa_kernel(tc, attn, Wo_bytes, Wo_scale, bo, query_inputs, gamma, beta, out):
@@ -89,9 +88,9 @@ def tile_multiheadattentionunit_pa_kernel(tc, attn, Wo_bytes, Wo_scale, bo, quer
         one = const.tile([P, 1], F32, name="one")
         nc.vector.memset(one[:], 1.0)
         one2 = const.tile([P, 1], F32, name="one2")
-        nc.scalar.activation(out=one2[:], in_=one[:], func=ACT.Sqrt)
+        nc.scalar.activation(out=one2[:], in_=one[:], func=ACT.Square)
 
-        minus_half = const.tile([P, 1], F32, name="minus_half")
+        minus_half = const.tile([P, 2], F32, name="minus_half")
         nc.gpsimd.memset(minus_half[:], -0.5)
 
         bcol = const.tile([P, 8 * H], F32, name="bcol")
@@ -258,9 +257,7 @@ def tile_multiheadattentionunit_pa_kernel(tc, attn, Wo_bytes, Wo_scale, bo, quer
                 interleave(k)
             else:
                 v_widen(8)
-            s_widen(2)
-            if k < 0:
-                s_widen(8)
+            s_widen(3)
             if has_a:
                 a_evac(a, 0)
             if ga:
@@ -273,7 +270,7 @@ def tile_multiheadattentionunit_pa_kernel(tc, attn, Wo_bytes, Wo_scale, bo, quer
             if gb:
                 empty(*gb[0])
                 product(gb[1][0], gb[1][1], ps_mx, "mxb")
-            s_widen(2)
+            s_widen(1)
             if has_k:
                 quant_w(k)
             if k == 0:
@@ -286,6 +283,7 @@ def tile_multiheadattentionunit_pa_kernel(tc, attn, Wo_bytes, Wo_scale, bo, quer
                 product(ga_next[0][0], ga_next[0][1], ps_mx, "mxa")
             if has_a:
                 a_evac(a, 1)
+            v_widen(1)
             if gb:
                 empty(*gb[1])
             if gb_next:
@@ -373,14 +371,14 @@ def tile_multiheadattentionunit_pa_kernel(tc, attn, Wo_bytes, Wo_scale, bo, quer
         add_up(13, 1)
         add_up(13, 2)
         add_up(13, 3)
-        empty(14, 0)
-        empty(14, 1)
         quant_w(15)
+        empty(14, 0)
         product(15, 0, ps_tr, "tr")
+        empty(14, 1)
         product(15, 1, ps_mx, "mxa")
         empty(14, 2)
-        empty(14, 3)
         product(15, 2, ps_tr, "tr")
+        empty(14, 3)
         product(15, 3, ps_mx, "mxb")
         empty(15, 0, "s")
         empty(15, 1, "v")
@@ -396,67 +394,63 @@ def tile_multiheadattentionunit_pa_kernel(tc, attn, Wo_bytes, Wo_scale, bo, quer
         turn_b(3, ps_mx, "mxb")
 
         out_rows = out.rearrange("b (j p) d -> (b j) p d", p=P)
-        stats = const.tile([P, NJ, 2, 6], F32, name="stats")
-        mv = const.tile([P, NJ, 2], F32, name="mv")
-        rstd = const.tile([P, NJ], F32, name="rstd")
-        s_sum = const.tile([P, 4], F32, name="s_sum")
-        g_val = const.tile([P, 8], F32, name="g_val")
-        junk = const.tile([P, HALF], F32, name="junk")
         halves = ((acc_a, 0), (acc_b, HALF))
+        stats = const.tile([P, 2, 2, 6], F32, name="stats")
+        mv = const.tile([P, 2, 2], F32, name="mv")
+        s_sum = const.tile([P, 2, 2], F32, name="s_sum")
+        s_sq = const.tile([P, 2, 2], F32, name="s_sq")
+        junk = const.tile([P, HALF], F32, name="junk")
+        ve01 = const.tile([P, 2], F32, name="ve01")
+        rstd01 = const.tile([P, 2], F32, name="rstd01")
+        nm32 = const.tile([P, 2], F32, name="nm32")
+        negmean23 = const.tile([P, 2], F32, name="negmean23")
+        ve23 = const.tile([P, 2], F32, name="ve23")
+        rstd23 = const.tile([P, 2], F32, name="rstd23")
 
-        def ln_stats(j):
-            nc.vector.bn_stats(out=stats[:, j, 1, :], in_=acc_b[j][:])
+        for i in range(2):
+            for j in range(2):
+                nc.vector.bn_stats(out=stats[:, j, i, :], in_=halves[i][0][j][:])
+                nc.scalar.activation(out=junk[:], in_=halves[i][0][2 + j][:], func=ACT.Identity, accum_out=s_sum[:, i, j : j + 1])
+        for j in range(2):
             nc.vector.bn_aggr(out=mv[:, j, :], in_=stats[:, j, :, :].rearrange("p a b -> p (a b)"))
-            nc.vector.tensor_scalar(out=rstd[:, j : j + 1], in0=mv[:, j, 1:2], scalar1=LN_EPS, scalar2=None, op0=ALU.add)
+        nc.gpsimd.tensor_scalar(out=ve01[:], in0=mv[:, :, 1], scalar1=1.0, scalar2=LN_EPS, op0=ALU.mult, op1=ALU.add)
+        nc.gpsimd.tensor_tensor(out=rstd01[:], in0=ve01[:], in1=minus_half[:], op=ALU.pow)
+        for j in range(2):
+            nc.gpsimd.tensor_scalar(out=nm32[:, j : j + 1], in0=s_sum[:, 0, j : j + 1], scalar1=s_sum[:, 1, j : j + 1],
+                                    scalar2=-1.0 / (32.0 * D), op0=ALU.add, op1=ALU.mult)
+            for i in range(2):
+                nc.scalar.activation(out=junk[:], in_=halves[i][0][2 + j][:], func=ACT.Square, scale=1.0 / 32.0, bias=nm32[:, j : j + 1],
+                                     accum_out=s_sq[:, i, j : j + 1])
+        nc.gpsimd.tensor_scalar(out=negmean23[:], in0=nm32[:], scalar1=32.0, scalar2=0.0, op0=ALU.mult, op1=ALU.add)
+        for j in range(2):
+            nc.gpsimd.tensor_scalar(out=ve23[:, j : j + 1], in0=s_sq[:, 0, j : j + 1], scalar1=s_sq[:, 1, j : j + 1], scalar2=LN_EPS,
+                                    op0=ALU.add, op1=ALU.add)
+        nc.gpsimd.tensor_tensor(out=rstd23[:], in0=ve23[:], in1=minus_half[:], op=ALU.pow)
 
-        def ln_sqrt(j):
-            nc.scalar.activation(out=rstd[:, j : j + 1], in_=rstd[:, j : j + 1], func=ACT.Sqrt)
+        cen = {}
 
-        def ln_apply(j):
-            nc.vector.reciprocal(out=rstd[:, j : j + 1], in_=rstd[:, j : j + 1])
-            cen = ln_pool.tile([P, D], F32, name="cen")
-            for acc, c0 in halves:
-                nc.vector.scalar_tensor_tensor(out=cen[:, c0 : c0 + HALF], in0=acc[j][:], scalar=mv[:, j, 0:1], in1=gam[:, c0 : c0 + HALF],
-                                               op0=ALU.subtract, op1=ALU.mult)
-            res = ln_pool.tile([P, D], F32, name="res")
-            if j < NJ - 1:
-                nc.vector.scalar_tensor_tensor(out=res[:], in0=cen[:], scalar=rstd[:, j : j + 1], in1=bet[:], op0=ALU.mult, op1=ALU.add)
-                nc.sync.dma_start(out=out_rows[j], in_=res[:])
+        def centre(j, i):
+            if j < 2:
+                shift, shift_op = mv[:, j, 0:1], ALU.subtract
             else:
-                for c0 in (0, HALF):
-                    nc.vector.scalar_tensor_tensor(out=res[:, c0 : c0 + HALF], in0=cen[:, c0 : c0 + HALF], scalar=rstd[:, j : j + 1],
-                                                   in1=bet[:, c0 : c0 + HALF], op0=ALU.mult, op1=ALU.add)
-                    nc.sync.dma_start(out=out_rows[j][:, c0 : c0 + HALF], in_=res[:, c0 : c0 + HALF])
+                shift, shift_op = negmean23[:, j - 2 : j - 1], ALU.add
+            if i == 0:
+                cen[j] = ln_pool.tile([P, D], F32, name="cen")
+            acc, c0 = halves[i]
+            nc.vector.scalar_tensor_tensor(out=cen[j][:, c0 : c0 + HALF], in0=acc[j][:], scalar=shift, in1=gam[:, c0 : c0 + HALF],
+                                           op0=shift_op, op1=ALU.mult)
 
-        for i in range(2):
-            nc.scalar.activation(out=junk[:], in_=halves[i][0][0][:], func=ACT.Identity, accum_out=s_sum[:, i : i + 1])
-        nc.gpsimd.tensor_tensor(out=g_val[:, 0:1], in0=s_sum[:, 0:1], in1=s_sum[:, 1:2], op=ALU.add)
-        nc.gpsimd.tensor_scalar(out=g_val[:, 1:2], in0=g_val[:, 0:1], scalar1=-1.0 / D, scalar2=0.0, op0=ALU.mult, op1=ALU.add)
-        for i in range(2):
-            nc.scalar.activation(out=junk[:], in_=halves[i][0][0][:], func=ACT.Square, bias=g_val[:, 1:2], accum_out=s_sum[:, 2 + i : 3 + i])
-        nc.gpsimd.tensor_tensor(out=g_val[:, 2:3], in0=s_sum[:, 2:3], in1=s_sum[:, 3:4], op=ALU.add)
-        nc.gpsimd.tensor_scalar(out=g_val[:, 3:4], in0=g_val[:, 2:3], scalar1=1.0 / D, scalar2=LN_EPS, op0=ALU.mult, op1=ALU.add)
-        nc.gpsimd.tensor_tensor(out=g_val[:, 4:5], in0=g_val[:, 3:4], in1=minus_half[:], op=ALU.pow)
-        nc.gpsimd.tensor_tensor(out=g_val[:, 5:6], in0=g_val[:, 1:2], in1=g_val[:, 4:5], op=ALU.mult)
+        def finish(j):
+            scale = rstd01[:, j : j + 1] if j < 2 else rstd23[:, j - 2 : j - 1]
+            res = ln_pool.tile([P, D], F32, name="res")
+            pieces = ((0, D),) if j < NJ - 1 else ((0, HALF), (HALF, D))
+            for c0, c1 in pieces:
+                nc.vector.scalar_tensor_tensor(out=res[:, c0:c1], in0=cen[j][:, c0:c1], scalar=scale, in1=bet[:, c0:c1], op0=ALU.mult, op1=ALU.add)
+                nc.sync.dma_start(out=out_rows[j][:, c0:c1], in_=res[:, c0:c1])
 
-        for j in range(1, NJ):
-            nc.vector.bn_stats(out=stats[:, j, 0, :], in_=acc_a[j][:])
-        ln_stats(1)
-        ln_sqrt(1)
-        ln_stats(2)
-        ln_sqrt(2)
-        norm0 = const.tile([P, D], F32, name="norm0")
-        res0 = const.tile([P, D], F32, name="res0")
-        for acc, c0 in halves:
-            nc.scalar.activation(out=norm0[:, c0 : c0 + HALF], in_=acc[0][:], func=ACT.Identity, scale=g_val[:, 4:5], bias=g_val[:, 5:6])
-        for c0 in range(0, D, GCH):
-            cols = slice(c0, c0 + GCH)
-            nc.gpsimd.tensor_tensor(out=norm0[:, cols], in0=norm0[:, cols], in1=gam[:, cols], op=ALU.mult)
-            nc.gpsimd.tensor_tensor(out=res0[:, cols], in0=norm0[:, cols], in1=bet[:, cols], op=ALU.add)
-        ln_apply(1)
-        ln_stats(3)
-        ln_sqrt(3)
-        for c0 in (0, HALF):
-            nc.scalar.dma_start(out=out_rows[0][:, c0 : c0 + HALF], in_=res0[:, c0 : c0 + HALF])
-        ln_apply(2)
-        ln_apply(3)
+        centre(0, 0)
+        for j in range(NJ):
+            centre(j, 1)
+            if j + 1 < NJ:
+                centre(j + 1, 0)
+            finish(j)

@@ -22,25 +22,29 @@ NTOK = B * S
 NJ = NTOK // P
 HALF = 512
 NPART = 2 * H
-WA = 3
+WA = 2
 
-V_WIDEN = {0: (1, 3, 4, 5, 7), 1: (3, 4, 5, 6, 7), 2: (4, 5, 6, 7), 3: (4, 5, 6, 7), 4: (5, 6, 7), 5: (5, 6, 7)}
-V_WIDEN_STEADY = {0: (6, 7), 1: (6, 7)}
+NV = {0: 5, 1: 5, 2: 5}
+NV1, NV2 = 5, 4
+SW = (1, 1, 1)
+VW = (2,)
+S_INTER = ()
+V_EMPTY = {15: (1, 3)}
 
 
 def tile_multiheadattentionunit_pa_kernel(tc, attn, Wo_bytes, Wo_scale, bo, query_inputs, gamma, beta, out):
     nc = tc.nc
     with ExitStack() as ctx:
         const = ctx.enter_context(tc.tile_pool(name="const", bufs=1))
-        wb_pool = ctx.enter_context(tc.tile_pool(name="wb", bufs=3))
-        wide_pool = ctx.enter_context(tc.tile_pool(name="wide", bufs=4))
+        wb_pool = ctx.enter_context(tc.tile_pool(name="wb", bufs=5))
+        wide_pool = ctx.enter_context(tc.tile_pool(name="wide", bufs=3))
         grp_pool = ctx.enter_context(tc.tile_pool(name="grp", bufs=2))
         wc_pool = ctx.enter_context(tc.tile_pool(name="wc", bufs=3))
         at_pool = ctx.enter_context(tc.tile_pool(name="at", bufs=6))
         ag_pool = ctx.enter_context(tc.tile_pool(name="ag", bufs=3))
-        ac_pool = ctx.enter_context(tc.tile_pool(name="ac", bufs=3))
-        r_pool = ctx.enter_context(tc.tile_pool(name="r", bufs=4))
-        ln_pool = ctx.enter_context(tc.tile_pool(name="ln", bufs=3))
+        r_pool = ctx.enter_context(tc.tile_pool(name="r", bufs=8))
+        cen_pool = ctx.enter_context(tc.tile_pool(name="cen", bufs=2))
+        res_pool = ctx.enter_context(tc.tile_pool(name="res", bufs=3))
         ps_acc = ctx.enter_context(tc.psum_pool(name="ps_acc", bufs=1))
         ps_mx = ctx.enter_context(tc.psum_pool(name="ps_mx", bufs=1))
         ps_tr = ctx.enter_context(tc.psum_pool(name="ps_tr", bufs=2))
@@ -48,15 +52,14 @@ def tile_multiheadattentionunit_pa_kernel(tc, attn, Wo_bytes, Wo_scale, bo, quer
 
         wb, wide, grp, wc, ws, at, ag, ac, asc = {}, {}, {}, {}, {}, {}, {}, {}, {}
 
-        def load_w(h):
-            wb[h] = wb_pool.tile([P, 8, D], U8, name="wbytes")
-            col_ranges = ((HALF, D), (0, HALF)) if h == 0 else ((0, D),)
-            for c0, c1 in col_ranges:
-                for g in range(2):
-                    nc.sync.dma_start(
-                        out=wb[h][:, 4 * g : 4 * g + 4, c0:c1],
-                        in_=Wo_bytes[h, 512 * g : 512 * (g + 1), c0:c1].rearrange("(p t) n -> p t n", t=4),
-                    )
+        def load_w(k):
+            s, h = divmod(k, H)
+            wb[k] = wb_pool.tile([P, 8, HALF], U8, name="wbytes")
+            for g in range(2):
+                nc.sync.dma_start(
+                    out=wb[k][:, 4 * g : 4 * g + 4, :],
+                    in_=Wo_bytes[h, 512 * g : 512 * (g + 1), HALF * s : HALF * (s + 1)].rearrange("(p t) n -> p t n", t=4),
+                )
 
         def load_a(h):
             for b in range(B):
@@ -71,14 +74,20 @@ def tile_multiheadattentionunit_pa_kernel(tc, attn, Wo_bytes, Wo_scale, bo, quer
         bo_rows = const.tile([P, P], BF16, name="bo_rows")
         nc.vector.memset(bo_rows[:], 0.0)
         nc.sync.dma_start(out=bo_rows[0 : 8 * H, :], in_=bo.rearrange("h (c p) -> (h c) p", p=P))
+        q_sb = const.tile([P, 2, NJ, HALF], BF16, name="q_sb")
+
+        def load_q(s):
+            nc.sync.dma_start(out=q_sb[:, s, :, :], in_=query_inputs[:, :, HALF * s : HALF * (s + 1)].rearrange("b (j p) d -> p (b j) d", p=P))
+
         load_w(0)
         load_a(0)
         load_w(1)
-        load_a(1)
         load_w(2)
-        q_sb = const.tile([P, NJ, D], BF16, name="q_sb")
-        nc.sync.dma_start(out=q_sb[:], in_=query_inputs.rearrange("b (j p) d -> p (b j) d", p=P))
+        load_a(1)
+        load_q(0)
+        load_w(3)
         load_a(2)
+        load_w(4)
 
         ident_f = const.tile([P, P], F32, name="ident_f")
         make_identity(nc, ident_f[:])
@@ -90,43 +99,45 @@ def tile_multiheadattentionunit_pa_kernel(tc, attn, Wo_bytes, Wo_scale, bo, quer
         one2 = const.tile([P, 1], F32, name="one2")
         nc.scalar.activation(out=one2[:], in_=one[:], func=ACT.Square)
 
-        minus_half = const.tile([P, 2], F32, name="minus_half")
+        minus_half = const.tile([P, 4], F32, name="minus_half")
         nc.gpsimd.memset(minus_half[:], -0.5)
 
         bcol = const.tile([P, 8 * H], F32, name="bcol")
         negb = const.tile([P, 8 * H], F32, name="negb")
-        btot = const.tile([P, 8], F32, name="btot")
-        acc_t = const.tile([P, 4, NTOK], F32, name="acc_t")
+        first_row = const.tile([P, P], BF16, name="first_row")
+        nc.vector.memset(first_row[:], 0.0)
+        nc.vector.memset(first_row[0:1, :], 1.0)
+        b_last = const.tile([P, HALF], BF16, name="b_last")
+        nc.vector.memset(b_last[:], 0.0)
+        x0 = const.tile([P, NJ, HALF], F32, name="x0")
         gam = const.tile([P, D], BF16, name="gam")
         bet = const.tile([P, D], BF16, name="bet")
-        acc_a = [ps_acc.tile([P, HALF], F32, name="acc_a%d" % j) for j in range(NJ)]
+        acc = [ps_acc.tile([P, HALF], F32, name="acc%d" % j) for j in range(NJ)]
+        for h in range(H):
+            ac[h] = const.tile([P, 2, NTOK], U32, name="acodes%d" % h, align_bytes=64)
+            asc[h] = const.tile([P, 2, NTOK], U8, name="ascales%d" % h, align_bytes=64)
 
         def prepare_bias():
             bo_t = ps_tr.tile([P, P], BF16, name="bo_t", tag="tr")
             nc.tensor.transpose(bo_t[:], bo_rows[:], ident_b[:])
             nc.vector.tensor_copy(out=bcol[:], in_=bo_t[:, 0 : 8 * H])
             nc.vector.tensor_scalar(out=negb[:], in0=bcol[:], scalar1=-1.0, scalar2=None, op0=ALU.mult)
-            nc.vector.tensor_reduce(out=btot[:], in_=bcol[:].rearrange("p (h c) -> p c h", h=H), axis=AX.X, op=ALU.add)
 
-        def open_acc():
+        def open_acc(s):
             for j in range(NJ):
-                nc.tensor.matmul(out=acc_a[j][:], lhsT=ident_b[:], rhs=q_sb[:, j, 0:HALF], start=True, stop=False)
+                nc.tensor.matmul(out=acc[j][:], lhsT=ident_b[:], rhs=q_sb[:, s, j, :], start=True, stop=False)
+                if s == 1:
+                    nc.tensor.matmul(out=acc[j][:], lhsT=first_row[:], rhs=b_last[:], start=False, stop=False)
 
         def widen(k, gt, eng):
-            h, s = divmod(k, 2)
-            c0 = HALF if s == 0 else 0
-            src = wb[h][:, gt, c0 : c0 + HALF].bitcast(FP8)
+            src = wb[k][:, gt, :].bitcast(FP8)
             if eng == "v":
                 nc.vector.tensor_scalar(out=wide[k][:, gt, :], in0=src, scalar1=w_scale[:, gt : gt + 1], scalar2=None, op0=ALU.mult)
             else:
                 nc.scalar.activation(out=wide[k][:, gt, :], in_=src, func=ACT.Copy, scale=w_scale[:, gt : gt + 1])
 
-        def interleave(k):
-            interleave_pass(k, 0, "v")
-            interleave_pass(k, 1, "v")
-
         def interleave_pass(k, g, eng):
-            if g == 0:
+            if k not in grp:
                 grp[k] = grp_pool.tile([P, 8 * HALF], BF16, name="grp", align_bytes=64)
             dst = grp[k][:, 4 * HALF * g : 4 * HALF * (g + 1)].rearrange("p (c i t) -> p c t i", i=4, t=4)
             src = wide[k][:, 4 * g : 4 * g + 4, :].rearrange("p t (c i) -> p c t i", i=4)
@@ -134,6 +145,20 @@ def tile_multiheadattentionunit_pa_kernel(tc, attn, Wo_bytes, Wo_scale, bo, quer
                 nc.vector.tensor_copy(out=dst, in_=src)
             else:
                 nc.scalar.copy(out=dst, in_=src)
+
+        def interleave_cols(k, g, n0, n1):
+            if k not in grp:
+                grp[k] = grp_pool.tile([P, 8 * HALF], BF16, name="grp", align_bytes=64)
+            dst = grp[k][:, 4 * (HALF * g + n0) : 4 * (HALF * g + n1)].rearrange("p (c i t) -> p c t i", i=4, t=4)
+            src = wide[k][:, 4 * g : 4 * g + 4, n0:n1].rearrange("p t (c i) -> p c t i", i=4)
+            nc.vector.tensor_copy(out=dst, in_=src)
+
+        def quant_cols(k, g, n0, n1):
+            if k not in wc:
+                wc[k] = wc_pool.tile([P, 2 * HALF], U32, name="wcodes", align_bytes=64)
+                ws[k] = wc_pool.tile([P, 2 * HALF], U8, name="wscales", align_bytes=64)
+            cols = slice(HALF * g + n0, HALF * g + n1)
+            nc.vector.quantize_mx(out=wc[k][:, cols].bitcast(FP8X4), scales=ws[k][:, cols], in_=grp[k][:, 4 * (HALF * g + n0) : 4 * (HALF * g + n1)])
 
         def quant_w(k):
             wc[k] = wc_pool.tile([P, 2 * HALF], U32, name="wcodes", align_bytes=64)
@@ -150,26 +175,25 @@ def tile_multiheadattentionunit_pa_kernel(tc, attn, Wo_bytes, Wo_scale, bo, quer
                 for u in range(2):
                     nc.tensor.transpose(xt[a, b][:, u, P * j : P * (j + 1)], words[:, 256 * g + u : 256 * (g + 1) : 2], ident_f[:])
 
-        def a_evac(a, b):
+        def a_evac(a, b, eng="s"):
             if b == 0:
                 ag[a] = ag_pool.tile([P, 4 * NTOK], BF16, name="agrp", align_bytes=64)
-            nc.scalar.copy(
-                out=ag[a][:, 1024 * b : 1024 * (b + 1)].bitcast(F32).rearrange("p (r u) -> p r u", u=2),
-                in_=xt[a, b][:].rearrange("p u r -> p r u"),
-            )
+            dst = ag[a][:, 1024 * b : 1024 * (b + 1)].bitcast(F32).rearrange("p (r u) -> p r u", u=2)
+            src = xt[a, b][:].rearrange("p u r -> p r u")
+            if eng == "s":
+                nc.scalar.copy(out=dst, in_=src)
+            else:
+                nc.vector.tensor_copy(out=dst, in_=src)
 
         def quant_a(a):
             h, g = divmod(a, 2)
-            if g == 0:
-                ac[h] = ac_pool.tile([P, 2, NTOK], U32, name="acodes", align_bytes=64)
-                asc[h] = ac_pool.tile([P, 2, NTOK], U8, name="ascales", align_bytes=64)
             nc.vector.quantize_mx(out=ac[h][:, g, :].bitcast(FP8X4), scales=asc[h][:, g, :], in_=ag[a][:])
 
         mx = {}
         r = {}
 
         def product(k, cc, pool, tag):
-            h = k // 2
+            h = k % H
             mx[k, cc] = pool.tile([P, NTOK], F32, name="mx", tag=tag)
             for g in range(2):
                 cols = slice(HALF * g + P * cc, HALF * g + P * (cc + 1))
@@ -184,220 +208,187 @@ def tile_multiheadattentionunit_pa_kernel(tc, attn, Wo_bytes, Wo_scale, bo, quer
                 )
 
         def empty(k, cc, eng="s"):
-            h, s = divmod(k, 2)
-            if s == 0:
-                col = 8 * h + 4 + cc
-                if h == 0:
-                    nc.vector.tensor_scalar(out=acc_t[:, cc, :], in0=mx[k, cc][:], scalar1=negb[:, col : col + 1],
-                                            scalar2=btot[:, 4 + cc : 5 + cc], op0=ALU.max, op1=ALU.add)
-                else:
-                    nc.vector.scalar_tensor_tensor(out=acc_t[:, cc, :], in0=mx[k, cc][:], scalar=negb[:, col : col + 1],
-                                                   in1=acc_t[:, cc, :], op0=ALU.max, op1=ALU.add)
+            s, h = divmod(k, H)
+            col = 8 * h + 4 * s + cc
+            r[k, cc] = r_pool.tile([P, NTOK], F32, name="relu")
+            if eng == "s":
+                nc.scalar.activation(out=r[k, cc][:], in_=mx[k, cc][:], func=ACT.Relu, bias=bcol[:, col : col + 1])
             else:
-                col = 8 * h + cc
-                r[k, cc] = r_pool.tile([P, NTOK], F32, name="relu")
-                if eng == "s":
-                    nc.scalar.activation(out=r[k, cc][:], in_=mx[k, cc][:], func=ACT.Relu, bias=bcol[:, col : col + 1])
-                else:
-                    nc.vector.tensor_scalar(out=r[k, cc][:], in0=mx[k, cc][:], scalar1=bcol[:, col : col + 1], scalar2=0.0,
-                                            op0=ALU.add, op1=ALU.max)
+                nc.vector.tensor_scalar(out=r[k, cc][:], in0=mx[k, cc][:], scalar1=bcol[:, col : col + 1], scalar2=0.0,
+                                        op0=ALU.add, op1=ALU.max)
+
+        def empty_onto(k, cc, k_before):
+            s, h = divmod(k, H)
+            col = 8 * h + 4 * s + cc
+            r[k, cc] = r_pool.tile([P, NTOK], F32, name="relu")
+            nc.vector.scalar_tensor_tensor(out=r[k, cc][:], in0=mx[k, cc][:], scalar=negb[:, col : col + 1], in1=r[k_before, cc][:],
+                                           op0=ALU.max, op1=ALU.add)
 
         def add_up(k, cc):
-            last = k == NPART - 1 and cc == 3
+            last = k % H == H - 1 and cc == 3
             for j in range(NJ):
-                nc.tensor.matmul(out=acc_a[j][:, P * cc : P * (cc + 1)], lhsT=r[k, cc][:, P * j : P * (j + 1)], rhs=ident_f[:],
+                nc.tensor.matmul(out=acc[j][:, P * cc : P * (cc + 1)], lhsT=r[k, cc][:, P * j : P * (j + 1)], rhs=ident_f[:],
                                  is_transpose=True, start=False, stop=last)
 
-        def groups(k):
-            pb = 2 * ((k - 1) // 2)
-            cb = (0, 1) if k % 2 == 1 else (2, 3)
-            pa = k - 1 if k % 2 == 0 else k - 2
-            ca = (0, 1) if k % 2 == 0 else (2, 3)
-            gb = [(pb, cc) for cc in cb] if 0 <= pb < NPART and k >= 1 else []
-            ga = [(pa, cc) for cc in ca] if 1 <= pa < NPART - 1 else []
-            return gb, ga
-
+        stats = const.tile([P, 2, 2, 6], F32, name="stats")
+        s_sum = const.tile([P, 2, 2], F32, name="s_sum")
         pending = []
 
-        def tick(k):
-            a, qa, kw = k + 2, k + 1, k + WA
-            has_a = 0 <= a < NPART
-            has_q = 0 <= qa < NPART
-            has_w = 0 <= kw < NPART
-            has_k = 0 <= k < NPART
-            gb, ga = groups(k)
-            gb_next, ga_next = groups(k + 1)
-            s_list = []
-            v_list = []
-            if has_w:
-                wide[kw] = wide_pool.tile([P, 8, HALF], BF16, name="wide")
-                v_list = list(V_WIDEN.get(kw, V_WIDEN_STEADY[kw % 2]))
-                s_list = [gt for gt in range(8) if gt not in v_list]
+        def which(k, cc):
+            return "v" if cc in V_EMPTY.get(k, ()) else "s"
 
-            def s_widen(n):
-                for gt in s_list[0:n]:
-                    widen(kw, gt, "s")
-                    s_list.remove(gt)
-
-            def v_widen(n):
-                for gt in v_list[0:n]:
-                    widen(kw, gt, "v")
-                    v_list.remove(gt)
-
-            if ga:
-                empty(*ga[0])
-            if has_a:
-                a_transpose(a, 0)
+        def flush():
             for item in pending:
                 add_up(*item)
             pending.clear()
-            if ga:
-                product(ga[1][0], ga[1][1], ps_mx, "mxa")
-            if has_k:
-                interleave(k)
-            else:
-                v_widen(8)
-            s_widen(3)
-            if has_a:
-                a_evac(a, 0)
-            if ga:
-                empty(*ga[1])
-                pending.append(ga[1])
-            if has_a:
-                a_transpose(a, 1)
-            if ga:
-                add_up(*ga[0])
-            if gb:
-                empty(*gb[0])
-                product(gb[1][0], gb[1][1], ps_mx, "mxb")
-            s_widen(1)
-            if has_k:
-                quant_w(k)
-            if k == 0:
-                for gt in V_WIDEN[2]:
-                    widen(2, gt, "v")
-                quant_a(0)
-            if has_q and qa > 0:
-                quant_a(qa)
-            if ga_next:
-                product(ga_next[0][0], ga_next[0][1], ps_mx, "mxa")
-            if has_a:
-                a_evac(a, 1)
-            v_widen(1)
-            if gb:
-                empty(*gb[1])
-            if gb_next:
-                product(gb_next[0][0], gb_next[0][1], ps_mx, "mxb")
-            s_widen(8)
-            v_widen(8)
-            if k >= 0 and k % 2 == 0 and k // 2 + 3 < H:
-                load_w(k // 2 + 3)
-                load_a(k // 2 + 3)
-            if k == 8:
+
+        def widen_lists(kw):
+            if not 0 <= kw < NPART:
+                return [], []
+            wide[kw] = wide_pool.tile([P, 8, HALF], BF16, name="wide")
+            nv = NV.get(kw, NV1 if kw < H + 2 else NV2)
+            return [(kw, gt, "s") for gt in range(8 - nv)], [(kw, gt, "v") for gt in range(8 - nv, 8)]
+
+        def some(rows, n):
+            for item in rows[0:n]:
+                widen(*item)
+                rows.remove(item)
+
+        def loads(t):
+            if t >= 0 and t + 5 < NPART:
+                load_w(t + 5)
+            if t == 4:
+                load_q(1)
+                nc.sync.dma_start(out=b_last[0:1, :], in_=bo[H - 1 : H, HALF:D])
+            if t >= 0 and t + 3 < H:
+                load_a(t + 3)
+            if t == 8:
                 nc.sync.dma_start(out=gam[:], in_=gamma.partition_broadcast(P))
                 nc.sync.dma_start(out=bet[:], in_=beta.partition_broadcast(P))
 
-        prepare_bias()
-        for kw in range(WA):
-            wide[kw] = wide_pool.tile([P, 8, HALF], BF16, name="wide")
-            for gt in range(8):
-                if gt not in V_WIDEN[kw]:
-                    widen(kw, gt, "s")
-            if kw < 2:
-                for gt in V_WIDEN[kw]:
-                    widen(kw, gt, "v")
-            if kw == 1:
-                for a in range(2):
-                    a_transpose(a, 0)
-                    a_transpose(a, 1)
-                    a_evac(a, 0)
-                    a_evac(a, 1)
-        tick(0)
-        tick(1)
-        open_acc()
-        for k in range(2, NPART - 3):
-            tick(k)
+        def tick1(t):
+            kp, ha = t - 1, t + 1
+            has_p, has_k = kp >= 0, t >= 0
+            s_rows, v_rows = widen_lists(t + WA)
+            flush()
+            if has_p:
+                product(kp, 0, ps_mx, "mxa")
+                product(kp, 1, ps_mx, "mxb")
+            if has_k:
+                interleave_pass(t, 0, "v")
+                interleave_pass(t, 1, "v")
+            some(s_rows, SW[0])
+            if has_p:
+                empty(kp, 0)
+                empty(kp, 1)
+            if ha >= 0:
+                a_transpose(2 * ha, 0)
+                a_transpose(2 * ha, 1)
+            if kp == 0:
+                open_acc(0)
+            if has_p:
+                add_up(kp, 0)
+                add_up(kp, 1)
+                product(kp, 2, ps_mx, "mxa")
+                product(kp, 3, ps_mx, "mxb")
+            some(s_rows, SW[1])
+            if has_k:
+                quant_a(2 * t)
+            some(v_rows, VW[0])
+            if ha >= 0:
+                a_evac(2 * ha, 0)
+                a_evac(2 * ha, 1)
+            some(s_rows, SW[2])
+            if has_k:
+                quant_w(t)
+            if has_p:
+                empty(kp, 2)
+                empty(kp, 3)
+                pending.append((kp, 2))
+                pending.append((kp, 3))
+            if ha >= 0:
+                a_transpose(2 * ha + 1, 0)
+                a_transpose(2 * ha + 1, 1)
+            some(s_rows, 8)
+            if has_k:
+                quant_a(2 * t + 1)
+            some(v_rows, 8)
+            if ha >= 0:
+                a_evac(2 * ha + 1, 0)
+                a_evac(2 * ha + 1, 1)
+            loads(t)
 
-        acc_b = {}
+        BANKS = ((ps_mx, "mxa"), (ps_mx, "mxb"), (ps_tr, "tr"), (ps_tr, "tr"))
 
-        def turn_b(j, pool, tag):
-            acc_b[j] = pool.tile([P, HALF], F32, name="acc_b", tag=tag)
-            nc.tensor.matmul(out=acc_b[j][:], lhsT=ident_b[:], rhs=q_sb[:, j, HALF:D], start=True, stop=False)
+        def tick2(t):
+            kp = t - 1
+            has_k = t < NPART
+            s_rows, v_rows = widen_lists(t + WA)
+            if kp == H:
+                flush()
+                for j in range(NJ):
+                    if j < 2:
+                        nc.scalar.copy(out=x0[:, j, :], in_=acc[j][:])
+                    else:
+                        nc.scalar.activation(out=x0[:, j, :], in_=acc[j][:], func=ACT.Identity, accum_out=s_sum[:, 0, j - 2 : j - 1])
             for cc in range(4):
-                nc.tensor.matmul(out=acc_b[j][:, P * cc : P * (cc + 1)], lhsT=acc_t[:, cc, P * j : P * (j + 1)], rhs=ident_f[:],
-                                 is_transpose=True, start=False, stop=(cc == 3))
+                product(kp, cc, *BANKS[cc])
+            flush()
+            if kp == H:
+                open_acc(1)
+            if t == NPART - 1:
+                Q = HALF // 2
+                interleave_cols(t, 0, 0, Q)
+                interleave_cols(t, 1, 0, Q)
+                interleave_cols(t, 0, Q, HALF)
+                quant_cols(t, 0, 0, Q)
+                quant_cols(t, 1, 0, Q)
+                interleave_cols(t, 1, Q, HALF)
+                for j in range(2):
+                    nc.vector.bn_stats(out=stats[:, j, 0, :], in_=x0[:, j, :])
+                quant_cols(t, 0, Q, HALF)
+                quant_cols(t, 1, Q, HALF)
+            elif has_k:
+                interleave_pass(t, 0, "v")
+                if t not in S_INTER:
+                    interleave_pass(t, 1, "v")
+                if t == H - 1:
+                    quant_a(2 * t)
+            some(v_rows, 1)
+            some(s_rows, 1)
+            if has_k and t < NPART - 1:
+                quant_w(t)
+                if t == H - 1:
+                    quant_a(2 * t + 1)
+            for cc in range(4):
+                if kp == NPART - 1:
+                    empty_onto(kp, cc, kp - 1)
+                    add_up(kp, cc)
+                else:
+                    empty(kp, cc)
+                    if kp < NPART - 2:
+                        if cc < 2:
+                            if cc == 1:
+                                some(s_rows, 2)
+                                add_up(kp, 0)
+                                add_up(kp, 1)
+                        else:
+                            pending.append((kp, cc))
+            some(v_rows, 8)
+            some(s_rows, 8)
+            if t + 2 in S_INTER:
+                interleave_pass(t + 2, 1, "s")
+            loads(t)
 
-        empty(11, 2)
-        a_transpose(15, 0)
-        for item in pending:
-            add_up(*item)
-        product(11, 3, ps_mx, "mxa")
-        interleave_pass(13, 0, "v")
-        interleave_pass(13, 1, "s")
-        a_evac(15, 0)
-        empty(11, 3)
-        a_transpose(15, 1)
-        add_up(11, 2)
-        add_up(11, 3)
-        empty(12, 0)
-        product(12, 1, ps_mx, "mxb")
-        interleave_pass(14, 0, "v")
-        interleave_pass(14, 1, "s")
-        quant_w(13)
-        quant_a(14)
-        product(13, 0, ps_mx, "mxa")
-        a_evac(15, 1)
-        empty(12, 1)
-        product(12, 2, ps_mx, "mxb")
-        product(12, 3, ps_tr, "tr")
-        empty(13, 0)
-        product(13, 1, ps_mx, "mxa")
-        add_up(13, 0)
-        interleave_pass(15, 0, "v")
-        interleave_pass(15, 1, "s")
-        quant_w(14)
-        quant_a(15)
-        empty(12, 2)
-        empty(12, 3)
-        product(13, 2, ps_tr, "tr")
-        product(13, 3, ps_mx, "mxb")
-        empty(13, 1)
-        empty(13, 2)
-        empty(13, 3)
-        product(14, 0, ps_tr, "tr")
-        product(14, 1, ps_mx, "mxa")
-        product(14, 2, ps_tr, "tr")
-        product(14, 3, ps_mx, "mxb")
-        add_up(13, 1)
-        add_up(13, 2)
-        add_up(13, 3)
-        quant_w(15)
-        empty(14, 0)
-        product(15, 0, ps_tr, "tr")
-        empty(14, 1)
-        product(15, 1, ps_mx, "mxa")
-        empty(14, 2)
-        product(15, 2, ps_tr, "tr")
-        empty(14, 3)
-        product(15, 3, ps_mx, "mxb")
-        empty(15, 0, "s")
-        empty(15, 1, "v")
-        empty(15, 2, "s")
-        empty(15, 3, "v")
-        add_up(15, 0)
-        add_up(15, 1)
-        add_up(15, 2)
-        add_up(15, 3)
-        turn_b(0, ps_tr, "tr")
-        turn_b(1, ps_mx, "mxa")
-        turn_b(2, ps_tr, "tr")
-        turn_b(3, ps_mx, "mxb")
+        prepare_bias()
+        for t in range(-WA, H - 1):
+            tick1(t)
+        for t in range(H - 1, NPART + 1):
+            tick2(t)
+        flush()
 
         out_rows = out.rearrange("b (j p) d -> (b j) p d", p=P)
-        halves = ((acc_a, 0), (acc_b, HALF))
-        stats = const.tile([P, 2, 2, 6], F32, name="stats")
         mv = const.tile([P, 2, 2], F32, name="mv")
-        s_sum = const.tile([P, 2, 2], F32, name="s_sum")
         s_sq = const.tile([P, 2, 2], F32, name="s_sq")
         junk = const.tile([P, HALF], F32, name="junk")
         ve01 = const.tile([P, 2], F32, name="ve01")
@@ -406,26 +397,24 @@ def tile_multiheadattentionunit_pa_kernel(tc, attn, Wo_bytes, Wo_scale, bo, quer
         negmean23 = const.tile([P, 2], F32, name="negmean23")
         ve23 = const.tile([P, 2], F32, name="ve23")
         rstd23 = const.tile([P, 2], F32, name="rstd23")
-
-        for i in range(2):
-            for j in range(2):
-                nc.vector.bn_stats(out=stats[:, j, i, :], in_=halves[i][0][j][:])
-                nc.scalar.activation(out=junk[:], in_=halves[i][0][2 + j][:], func=ACT.Identity, accum_out=s_sum[:, i, j : j + 1])
+        for j in range(2):
+            nc.vector.bn_stats(out=stats[:, j, 1, :], in_=acc[j][:])
+            nc.scalar.activation(out=junk[:], in_=acc[2 + j][:], func=ACT.Identity, accum_out=s_sum[:, 1, j : j + 1])
         for j in range(2):
             nc.vector.bn_aggr(out=mv[:, j, :], in_=stats[:, j, :, :].rearrange("p a b -> p (a b)"))
         nc.gpsimd.tensor_scalar(out=ve01[:], in0=mv[:, :, 1], scalar1=1.0, scalar2=LN_EPS, op0=ALU.mult, op1=ALU.add)
-        nc.gpsimd.tensor_tensor(out=rstd01[:], in0=ve01[:], in1=minus_half[:], op=ALU.pow)
+        nc.gpsimd.tensor_tensor(out=rstd01[:], in0=ve01[:], in1=minus_half[:, 0:2], op=ALU.pow)
         for j in range(2):
             nc.gpsimd.tensor_scalar(out=nm32[:, j : j + 1], in0=s_sum[:, 0, j : j + 1], scalar1=s_sum[:, 1, j : j + 1],
                                     scalar2=-1.0 / (32.0 * D), op0=ALU.add, op1=ALU.mult)
             for i in range(2):
-                nc.scalar.activation(out=junk[:], in_=halves[i][0][2 + j][:], func=ACT.Square, scale=1.0 / 32.0, bias=nm32[:, j : j + 1],
-                                     accum_out=s_sq[:, i, j : j + 1])
+                nc.scalar.activation(out=junk[:], in_=(x0[:, 2 + j, :] if i == 0 else acc[2 + j][:]), func=ACT.Square, scale=1.0 / 32.0,
+                                     bias=nm32[:, j : j + 1], accum_out=s_sq[:, i, j : j + 1])
         nc.gpsimd.tensor_scalar(out=negmean23[:], in0=nm32[:], scalar1=32.0, scalar2=0.0, op0=ALU.mult, op1=ALU.add)
         for j in range(2):
             nc.gpsimd.tensor_scalar(out=ve23[:, j : j + 1], in0=s_sq[:, 0, j : j + 1], scalar1=s_sq[:, 1, j : j + 1], scalar2=LN_EPS,
                                     op0=ALU.add, op1=ALU.add)
-        nc.gpsimd.tensor_tensor(out=rstd23[:], in0=ve23[:], in1=minus_half[:], op=ALU.pow)
+        nc.gpsimd.tensor_tensor(out=rstd23[:], in0=ve23[:], in1=minus_half[:, 0:2], op=ALU.pow)
 
         cen = {}
 
@@ -435,17 +424,19 @@ def tile_multiheadattentionunit_pa_kernel(tc, attn, Wo_bytes, Wo_scale, bo, quer
             else:
                 shift, shift_op = negmean23[:, j - 2 : j - 1], ALU.add
             if i == 0:
-                cen[j] = ln_pool.tile([P, D], F32, name="cen")
-            acc, c0 = halves[i]
-            nc.vector.scalar_tensor_tensor(out=cen[j][:, c0 : c0 + HALF], in0=acc[j][:], scalar=shift, in1=gam[:, c0 : c0 + HALF],
+                cen[j] = cen_pool.tile([P, D], F32, name="cen")
+            src = x0[:, j, :] if i == 0 else acc[j][:]
+            c0 = HALF * i
+            nc.vector.scalar_tensor_tensor(out=cen[j][:, c0 : c0 + HALF], in0=src, scalar=shift, in1=gam[:, c0 : c0 + HALF],
                                            op0=shift_op, op1=ALU.mult)
 
         def finish(j):
             scale = rstd01[:, j : j + 1] if j < 2 else rstd23[:, j - 2 : j - 1]
-            res = ln_pool.tile([P, D], F32, name="res")
+            res = res_pool.tile([P, D], F32, name="res")
             pieces = ((0, D),) if j < NJ - 1 else ((0, HALF), (HALF, D))
             for c0, c1 in pieces:
-                nc.vector.scalar_tensor_tensor(out=res[:, c0:c1], in0=cen[j][:, c0:c1], scalar=scale, in1=bet[:, c0:c1], op0=ALU.mult, op1=ALU.add)
+                nc.vector.scalar_tensor_tensor(out=res[:, c0:c1], in0=cen[j][:, c0:c1], scalar=scale, in1=bet[:, c0:c1],
+                                               op0=ALU.mult, op1=ALU.add)
                 nc.sync.dma_start(out=out_rows[j][:, c0:c1], in_=res[:, c0:c1])
 
         centre(0, 0)

@@ -24,10 +24,12 @@ HALF = 512
 NPART = 2 * H
 WA = 2
 
-NV = {0: 5, 1: 5, 2: 5}
+NV = {0: 5, 1: 5, 2: 5, 11: 6}
 NV1, NV2 = 5, 4
 SW = (1, 1, 1)
 VW = (2,)
+DOUBLE_AT = 0
+MERGE = (0, 1, 2, 3)
 S_INTER = ()
 V_EMPTY = {15: (1, 3)}
 
@@ -242,12 +244,15 @@ def tile_multiheadattentionunit_pa_kernel(tc, attn, Wo_bytes, Wo_scale, bo, quer
                 add_up(*item)
             pending.clear()
 
-        def widen_lists(kw):
-            if not 0 <= kw < NPART:
-                return [], []
-            wide[kw] = wide_pool.tile([P, 8, HALF], BF16, name="wide")
-            nv = NV.get(kw, NV1 if kw < H + 2 else NV2)
-            return [(kw, gt, "s") for gt in range(8 - nv)], [(kw, gt, "v") for gt in range(8 - nv, 8)]
+        def widen_lists(t):
+            s_rows, v_rows = [], []
+            for kw in ((t + 1,) if t < DOUBLE_AT else (t + 1, t + 2) if t == DOUBLE_AT else (t + 2,)):
+                if kw < NPART:
+                    wide[kw] = wide_pool.tile([P, 8, HALF], BF16, name="wide")
+                    nv = NV.get(kw, NV1 if kw < H + 2 else NV2)
+                    s_rows.extend((kw, gt, "s") for gt in range(8 - nv))
+                    v_rows.extend((kw, gt, "v") for gt in range(8 - nv, 8))
+            return s_rows, v_rows
 
         def some(rows, n):
             for item in rows[0:n]:
@@ -259,7 +264,8 @@ def tile_multiheadattentionunit_pa_kernel(tc, attn, Wo_bytes, Wo_scale, bo, quer
                 load_w(t + 5)
             if t == 4:
                 load_q(1)
-                nc.sync.dma_start(out=b_last[0:1, :], in_=bo[H - 1 : H, HALF:D])
+                for cc in MERGE:
+                    nc.sync.dma_start(out=b_last[0:1, P * cc : P * (cc + 1)], in_=bo[H - 1 : H, HALF + P * cc : HALF + P * (cc + 1)])
             if t >= 0 and t + 3 < H:
                 load_a(t + 3)
             if t == 8:
@@ -269,7 +275,7 @@ def tile_multiheadattentionunit_pa_kernel(tc, attn, Wo_bytes, Wo_scale, bo, quer
         def tick1(t):
             kp, ha = t - 1, t + 1
             has_p, has_k = kp >= 0, t >= 0
-            s_rows, v_rows = widen_lists(t + WA)
+            s_rows, v_rows = widen_lists(t)
             flush()
             if has_p:
                 product(kp, 0, ps_mx, "mxa")
@@ -277,7 +283,7 @@ def tile_multiheadattentionunit_pa_kernel(tc, attn, Wo_bytes, Wo_scale, bo, quer
             if has_k:
                 interleave_pass(t, 0, "v")
                 interleave_pass(t, 1, "v")
-            some(s_rows, SW[0])
+            some(s_rows, SW[0] if has_p else 3)
             if has_p:
                 empty(kp, 0)
                 empty(kp, 1)
@@ -292,6 +298,8 @@ def tile_multiheadattentionunit_pa_kernel(tc, attn, Wo_bytes, Wo_scale, bo, quer
                 product(kp, 2, ps_mx, "mxa")
                 product(kp, 3, ps_mx, "mxb")
             some(s_rows, SW[1])
+            if t == DOUBLE_AT:
+                some(v_rows, 5)
             if has_k:
                 quant_a(2 * t)
             some(v_rows, VW[0])
@@ -323,7 +331,7 @@ def tile_multiheadattentionunit_pa_kernel(tc, attn, Wo_bytes, Wo_scale, bo, quer
         def tick2(t):
             kp = t - 1
             has_k = t < NPART
-            s_rows, v_rows = widen_lists(t + WA)
+            s_rows, v_rows = widen_lists(t)
             if kp == H:
                 flush()
                 for j in range(NJ):
@@ -362,11 +370,14 @@ def tile_multiheadattentionunit_pa_kernel(tc, attn, Wo_bytes, Wo_scale, bo, quer
                     quant_a(2 * t + 1)
             for cc in range(4):
                 if kp == NPART - 1:
-                    empty_onto(kp, cc, kp - 1)
+                    if cc in MERGE:
+                        empty_onto(kp, cc, kp - 1)
+                    else:
+                        empty(kp, cc)
                     add_up(kp, cc)
                 else:
                     empty(kp, cc)
-                    if kp < NPART - 2:
+                    if kp < NPART - 2 or cc not in MERGE:
                         if cc < 2:
                             if cc == 1:
                                 some(s_rows, 2)
@@ -381,7 +392,7 @@ def tile_multiheadattentionunit_pa_kernel(tc, attn, Wo_bytes, Wo_scale, bo, quer
             loads(t)
 
         prepare_bias()
-        for t in range(-WA, H - 1):
+        for t in range(-1, H - 1):
             tick1(t)
         for t in range(H - 1, NPART + 1):
             tick2(t)

@@ -28,6 +28,7 @@ NV = {0: 5, 1: 5, 2: 5, 11: 6}
 NV1, NV2 = 5, 4
 SW = (1, 1, 1)
 VW = (2,)
+STORE_AFTER = 0
 DOUBLE_AT = 0
 MERGE = (0, 1, 2, 3)
 S_INTER = ()
@@ -76,6 +77,8 @@ def tile_multiheadattentionunit_pa_kernel(tc, attn, Wo_bytes, Wo_scale, bo, quer
         bo_rows = const.tile([P, P], BF16, name="bo_rows")
         nc.vector.memset(bo_rows[:], 0.0)
         nc.sync.dma_start(out=bo_rows[0 : 8 * H, :], in_=bo.rearrange("h (c p) -> (h c) p", p=P))
+        nc.sync.dma_start(out=bo_rows[8 * H : 8 * H + 8, :], in_=gamma.rearrange("(c p) -> c p", p=P))
+        nc.sync.dma_start(out=bo_rows[8 * H + 8 : 8 * H + 16, :], in_=beta.rearrange("(c p) -> c p", p=P))
         q_sb = const.tile([P, 2, NJ, HALF], BF16, name="q_sb")
 
         def load_q(s):
@@ -104,7 +107,7 @@ def tile_multiheadattentionunit_pa_kernel(tc, attn, Wo_bytes, Wo_scale, bo, quer
         minus_half = const.tile([P, 4], F32, name="minus_half")
         nc.gpsimd.memset(minus_half[:], -0.5)
 
-        bcol = const.tile([P, 8 * H], F32, name="bcol")
+        bcol = const.tile([P, 8 * H + 16], F32, name="bcol")
         negb = const.tile([P, 8 * H], F32, name="negb")
         first_row = const.tile([P, P], BF16, name="first_row")
         nc.vector.memset(first_row[:], 0.0)
@@ -122,8 +125,8 @@ def tile_multiheadattentionunit_pa_kernel(tc, attn, Wo_bytes, Wo_scale, bo, quer
         def prepare_bias():
             bo_t = ps_tr.tile([P, P], BF16, name="bo_t", tag="tr")
             nc.tensor.transpose(bo_t[:], bo_rows[:], ident_b[:])
-            nc.vector.tensor_copy(out=bcol[:], in_=bo_t[:, 0 : 8 * H])
-            nc.vector.tensor_scalar(out=negb[:], in0=bcol[:], scalar1=-1.0, scalar2=None, op0=ALU.mult)
+            nc.vector.tensor_copy(out=bcol[:], in_=bo_t[:, 0 : 8 * H + 16])
+            nc.vector.tensor_scalar(out=negb[:], in0=bcol[:, 0 : 8 * H], scalar1=-1.0, scalar2=None, op0=ALU.mult)
 
         def open_acc(s):
             for j in range(NJ):
@@ -232,8 +235,11 @@ def tile_multiheadattentionunit_pa_kernel(tc, attn, Wo_bytes, Wo_scale, bo, quer
                 nc.tensor.matmul(out=acc[j][:, P * cc : P * (cc + 1)], lhsT=r[k, cc][:, P * j : P * (j + 1)], rhs=ident_f[:],
                                  is_transpose=True, start=False, stop=last)
 
-        stats = const.tile([P, 2, 2, 6], F32, name="stats")
-        s_sum = const.tile([P, 2, 2], F32, name="s_sum")
+        rec = const.tile([P, NJ, 3, 8], F32, name="rec")
+        nc.gpsimd.memset(rec[:], float(HALF))
+        s_sum = const.tile([P, 2, NJ], F32, name="s_sum")
+        negm = const.tile([P, 2, NJ], F32, name="negm")
+        junk = const.tile([P, HALF], F32, name="junk")
         pending = []
 
         def which(k, cc):
@@ -335,10 +341,9 @@ def tile_multiheadattentionunit_pa_kernel(tc, attn, Wo_bytes, Wo_scale, bo, quer
             if kp == H:
                 flush()
                 for j in range(NJ):
-                    if j < 2:
-                        nc.scalar.copy(out=x0[:, j, :], in_=acc[j][:])
-                    else:
-                        nc.scalar.activation(out=x0[:, j, :], in_=acc[j][:], func=ACT.Identity, accum_out=s_sum[:, 0, j - 2 : j - 1])
+                    nc.scalar.activation(out=x0[:, j, :], in_=acc[j][:], func=ACT.Identity, accum_out=s_sum[:, 0, j : j + 1])
+                nc.gpsimd.tensor_scalar(out=rec[:, :, 0, 1], in0=s_sum[:, 0, :], scalar1=1.0 / HALF, scalar2=0.0, op0=ALU.mult, op1=ALU.add)
+                nc.gpsimd.tensor_scalar(out=negm[:, 0, :], in0=s_sum[:, 0, :], scalar1=-1.0 / HALF, scalar2=0.0, op0=ALU.mult, op1=ALU.add)
             for cc in range(4):
                 product(kp, cc, *BANKS[cc])
             flush()
@@ -352,8 +357,6 @@ def tile_multiheadattentionunit_pa_kernel(tc, attn, Wo_bytes, Wo_scale, bo, quer
                 quant_cols(t, 0, 0, Q)
                 quant_cols(t, 1, 0, Q)
                 interleave_cols(t, 1, Q, HALF)
-                for j in range(2):
-                    nc.vector.bn_stats(out=stats[:, j, 0, :], in_=x0[:, j, :])
                 quant_cols(t, 0, Q, HALF)
                 quant_cols(t, 1, Q, HALF)
             elif has_k:
@@ -387,8 +390,9 @@ def tile_multiheadattentionunit_pa_kernel(tc, attn, Wo_bytes, Wo_scale, bo, quer
                             pending.append((kp, cc))
             some(v_rows, 8)
             some(s_rows, 8)
-            if t + 2 in S_INTER:
-                interleave_pass(t + 2, 1, "s")
+            if t in (NPART - 2, NPART - 1):
+                for j in ((0, 1) if t == NPART - 2 else (2, 3)):
+                    nc.scalar.activation(out=junk[:], in_=x0[:, j, :], func=ACT.Square, bias=negm[:, 0, j : j + 1], accum_out=rec[:, j, 0, 2:3])
             loads(t)
 
         prepare_bias()
@@ -399,60 +403,79 @@ def tile_multiheadattentionunit_pa_kernel(tc, attn, Wo_bytes, Wo_scale, bo, quer
         flush()
 
         out_rows = out.rearrange("b (j p) d -> (b j) p d", p=P)
-        mv = const.tile([P, 2, 2], F32, name="mv")
-        s_sq = const.tile([P, 2, 2], F32, name="s_sq")
-        junk = const.tile([P, HALF], F32, name="junk")
-        ve01 = const.tile([P, 2], F32, name="ve01")
-        rstd01 = const.tile([P, 2], F32, name="rstd01")
-        nm32 = const.tile([P, 2], F32, name="nm32")
-        negmean23 = const.tile([P, 2], F32, name="negmean23")
-        ve23 = const.tile([P, 2], F32, name="ve23")
-        rstd23 = const.tile([P, 2], F32, name="rstd23")
-        for j in range(2):
-            nc.vector.bn_stats(out=stats[:, j, 1, :], in_=acc[j][:])
-            nc.scalar.activation(out=junk[:], in_=acc[2 + j][:], func=ACT.Identity, accum_out=s_sum[:, 1, j : j + 1])
-        for j in range(2):
-            nc.vector.bn_aggr(out=mv[:, j, :], in_=stats[:, j, :, :].rearrange("p a b -> p (a b)"))
-        nc.gpsimd.tensor_scalar(out=ve01[:], in0=mv[:, :, 1], scalar1=1.0, scalar2=LN_EPS, op0=ALU.mult, op1=ALU.add)
-        nc.gpsimd.tensor_tensor(out=rstd01[:], in0=ve01[:], in1=minus_half[:, 0:2], op=ALU.pow)
-        for j in range(2):
-            nc.gpsimd.tensor_scalar(out=nm32[:, j : j + 1], in0=s_sum[:, 0, j : j + 1], scalar1=s_sum[:, 1, j : j + 1],
-                                    scalar2=-1.0 / (32.0 * D), op0=ALU.add, op1=ALU.mult)
-            for i in range(2):
-                nc.scalar.activation(out=junk[:], in_=(x0[:, 2 + j, :] if i == 0 else acc[2 + j][:]), func=ACT.Square, scale=1.0 / 32.0,
-                                     bias=nm32[:, j : j + 1], accum_out=s_sq[:, i, j : j + 1])
-        nc.gpsimd.tensor_scalar(out=negmean23[:], in0=nm32[:], scalar1=32.0, scalar2=0.0, op0=ALU.mult, op1=ALU.add)
-        for j in range(2):
-            nc.gpsimd.tensor_scalar(out=ve23[:, j : j + 1], in0=s_sq[:, 0, j : j + 1], scalar1=s_sq[:, 1, j : j + 1], scalar2=LN_EPS,
-                                    op0=ALU.add, op1=ALU.add)
-        nc.gpsimd.tensor_tensor(out=rstd23[:], in0=ve23[:], in1=minus_half[:, 0:2], op=ALU.pow)
+        mv = const.tile([P, NJ, 2], F32, name="mv")
+        ve = const.tile([P, NJ], F32, name="ve")
+        rstd = const.tile([P, NJ], F32, name="rstd")
+
+        def scalar_sum(j):
+            nc.scalar.activation(out=junk[:], in_=acc[j][:], func=ACT.Identity, accum_out=s_sum[:, 1, j : j + 1])
+            nc.scalar.activation(out=negm[:, 1, j : j + 1], in_=s_sum[:, 1, j : j + 1], func=ACT.Copy, scale=-1.0 / HALF)
+            nc.scalar.activation(out=rec[:, j, 1, 1:2], in_=s_sum[:, 1, j : j + 1], func=ACT.Copy, scale=1.0 / HALF)
+
+        def scalar_squares(j):
+            nc.scalar.activation(out=junk[:], in_=acc[j][:], func=ACT.Square, bias=negm[:, 1, j : j + 1], accum_out=rec[:, j, 1, 2:3])
+
+        def aggregate(j, n):
+            nc.vector.bn_aggr(out=mv[:, j, :], in_=rec[:, j, 0:n, 0:3])
+            nc.gpsimd.tensor_scalar(out=ve[:, j : j + 1], in0=mv[:, j, 1:2], scalar1=1.0, scalar2=LN_EPS, op0=ALU.mult, op1=ALU.add)
+            nc.gpsimd.tensor_tensor(out=rstd[:, j : j + 1], in0=ve[:, j : j + 1], in1=minus_half[:, 0:1], op=ALU.pow)
+
+        LAST = NJ - 1
+        nmr = const.tile([P, 1], F32, name="nmr")
+        nc.vector.bn_stats(out=rec[:, LAST, 1:3, 0:3], in_=acc[LAST][:])
+        scalar_sum(2)
+        aggregate(LAST, 3)
+        nc.gpsimd.tensor_scalar(out=nmr[:], in0=mv[:, LAST, 0:1], scalar1=rstd[:, LAST : LAST + 1], scalar2=-1.0, op0=ALU.mult, op1=ALU.mult)
+        nc.vector.bn_stats(out=rec[:, 0, 1:3, 0:3], in_=acc[0][:])
+        nc.vector.bn_stats(out=rec[:, 1, 1:3, 0:3], in_=acc[1][:])
+        scalar_squares(2)
+        aggregate(0, 3)
+
+        norm = const.tile([P, D], F32, name="norm")
+        turned = const.tile([P, 8, P], F32, name="turned")
+        res_last = const.tile([P, D], F32, name="res_last")
+        for i in range(2):
+            nc.scalar.activation(out=norm[:, HALF * i : HALF * (i + 1)], in_=(x0[:, LAST, :] if i == 0 else acc[LAST][:]), func=ACT.Identity,
+                                 scale=rstd[:, LAST : LAST + 1], bias=nmr[:])
+        for i in range(2):
+            there = ps_mx.tile([P, 4, P], F32, name="there", tag=("mxa", "mxb")[i])
+            for c in range(4):
+                nc.tensor.transpose(there[:, c, :], norm[:, HALF * i + P * c : HALF * i + P * (c + 1)], ident_f[:])
+            for c in range(4):
+                col = 8 * H + 4 * i + c
+                nc.scalar.activation(out=turned[:, 4 * i + c, :], in_=there[:, c, :], func=ACT.Identity, scale=bcol[:, col : col + 1],
+                                     bias=bcol[:, col + 8 : col + 9])
+        for i in range(2):
+            back = ps_tr.tile([P, 4, P], F32, name="back", tag="tr")
+            for c in range(4):
+                nc.tensor.transpose(back[:, c, :], turned[:, 4 * i + c, :], ident_f[:])
+            nc.scalar.copy(out=res_last[:, HALF * i : HALF * (i + 1)], in_=back[:].rearrange("p c t -> p (c t)"))
+            nc.scalar.dma_start(out=out_rows[LAST][:, HALF * i : HALF * (i + 1)], in_=res_last[:, HALF * i : HALF * (i + 1)])
 
         cen = {}
 
         def centre(j, i):
-            if j < 2:
-                shift, shift_op = mv[:, j, 0:1], ALU.subtract
-            else:
-                shift, shift_op = negmean23[:, j - 2 : j - 1], ALU.add
             if i == 0:
                 cen[j] = cen_pool.tile([P, D], F32, name="cen")
             src = x0[:, j, :] if i == 0 else acc[j][:]
             c0 = HALF * i
-            nc.vector.scalar_tensor_tensor(out=cen[j][:, c0 : c0 + HALF], in0=src, scalar=shift, in1=gam[:, c0 : c0 + HALF],
-                                           op0=shift_op, op1=ALU.mult)
+            nc.vector.scalar_tensor_tensor(out=cen[j][:, c0 : c0 + HALF], in0=src, scalar=mv[:, j, 0:1], in1=gam[:, c0 : c0 + HALF],
+                                           op0=ALU.subtract, op1=ALU.mult)
 
         def finish(j):
-            scale = rstd01[:, j : j + 1] if j < 2 else rstd23[:, j - 2 : j - 1]
+            scale = rstd[:, j : j + 1]
             res = res_pool.tile([P, D], F32, name="res")
-            pieces = ((0, D),) if j < NJ - 1 else ((0, HALF), (HALF, D))
+            pieces = ((0, D),) if j < NJ - 2 else ((0, HALF), (HALF, D))
             for c0, c1 in pieces:
                 nc.vector.scalar_tensor_tensor(out=res[:, c0:c1], in0=cen[j][:, c0:c1], scalar=scale, in1=bet[:, c0:c1],
                                                op0=ALU.mult, op1=ALU.add)
                 nc.sync.dma_start(out=out_rows[j][:, c0:c1], in_=res[:, c0:c1])
 
         centre(0, 0)
-        for j in range(NJ):
+        for j in range(LAST):
+            if j + 1 < LAST:
+                aggregate(j + 1, 3 if j + 1 < 2 else 2)
             centre(j, 1)
-            if j + 1 < NJ:
+            if j + 1 < LAST:
                 centre(j + 1, 0)
             finish(j)

@@ -74,6 +74,7 @@ def tile_multiheadattentionunit_pa_kernel(tc, attn, Wo_bytes, Wo_scale, bo, quer
             out=w_scale[:].rearrange("p (g t) -> p g t", g=2),
             in_=Wo_scale.rearrange("o (g p t) x -> p (o g) (t x)", g=2, p=P, t=4),
         )
+        load_w(0)
         bo_rows = const.tile([P, P], BF16, name="bo_rows")
         nc.vector.memset(bo_rows[:], 0.0)
         nc.sync.dma_start(out=bo_rows[0 : 8 * H, :], in_=bo.rearrange("h (c p) -> (h c) p", p=P))
@@ -84,7 +85,6 @@ def tile_multiheadattentionunit_pa_kernel(tc, attn, Wo_bytes, Wo_scale, bo, quer
         def load_q(s):
             nc.sync.dma_start(out=q_sb[:, s, :, :], in_=query_inputs[:, :, HALF * s : HALF * (s + 1)].rearrange("b (j p) d -> p (b j) d", p=P))
 
-        load_w(0)
         load_a(0)
         load_w(1)
         load_w(2)
@@ -122,9 +122,9 @@ def tile_multiheadattentionunit_pa_kernel(tc, attn, Wo_bytes, Wo_scale, bo, quer
             ac[h] = const.tile([P, 2, NTOK], U32, name="acodes%d" % h, align_bytes=64)
             asc[h] = const.tile([P, 2, NTOK], U8, name="ascales%d" % h, align_bytes=64)
 
+        bo_t = ps_mx.tile([P, P], BF16, name="bo_t", tag="mxa")
+
         def prepare_bias():
-            bo_t = ps_tr.tile([P, P], BF16, name="bo_t", tag="tr")
-            nc.tensor.transpose(bo_t[:], bo_rows[:], ident_b[:])
             nc.vector.tensor_copy(out=bcol[:], in_=bo_t[:, 0 : 8 * H + 16])
             nc.vector.tensor_scalar(out=negb[:], in0=bcol[:, 0 : 8 * H], scalar1=-1.0, scalar2=None, op0=ALU.mult)
 
@@ -231,7 +231,7 @@ def tile_multiheadattentionunit_pa_kernel(tc, attn, Wo_bytes, Wo_scale, bo, quer
 
         def add_up(k, cc):
             last = k % H == H - 1 and cc == 3
-            for j in range(NJ):
+            for j in ((3, 0, 1, 2) if last else range(NJ)):
                 nc.tensor.matmul(out=acc[j][:, P * cc : P * (cc + 1)], lhsT=r[k, cc][:, P * j : P * (j + 1)], rhs=ident_f[:],
                                  is_transpose=True, start=False, stop=last)
 
@@ -395,8 +395,10 @@ def tile_multiheadattentionunit_pa_kernel(tc, attn, Wo_bytes, Wo_scale, bo, quer
                     nc.scalar.activation(out=junk[:], in_=x0[:, j, :], func=ACT.Square, bias=negm[:, 0, j : j + 1], accum_out=rec[:, j, 0, 2:3])
             loads(t)
 
+        nc.tensor.transpose(bo_t[:], bo_rows[:], ident_b[:])
+        tick1(-1)
         prepare_bias()
-        for t in range(-1, H - 1):
+        for t in range(0, H - 1):
             tick1(t)
         for t in range(H - 1, NPART + 1):
             tick2(t)

@@ -24,8 +24,18 @@ HALF = 512
 NPART = 2 * H
 WA = 2
 
-NV = {0: 5, 1: 5, 2: 5, 11: 6}
+NV = {0: 5, 1: 5, 2: 5, 11: 6, 13: 4, 14: 3, 15: 3}
 NV1, NV2 = 5, 4
+PASSES_APART = (0, NPART - 1)
+SPLIT = (NPART - 1,)
+VFIRST = {0: (0, 1, 2, 3, 4), 15: (0, 1, 2, 3)}
+S1 = {}
+S2 = {}
+LASTORD = {15: (("i", 0, 0), ("i", 0, 1), ("i", 1, 0), ("q", 0, 0), ("q", 1, 0), ("i", 1, 1), ("q", 0, 1), ("q", 1, 1))}
+
+WIDEN_AT = {15: 14}
+SQ = {15: (0, 1), 16: (2, 3)}
+
 SW = (1, 1, 1)
 VW = (2,)
 STORE_AFTER = 0
@@ -136,10 +146,11 @@ def tile_multiheadattentionunit_pa_kernel(tc, attn, Wo_bytes, Wo_scale, bo, quer
 
         def widen(k, gt, eng):
             src = wb[k][:, gt, :].bitcast(FP8)
+            dst = wide[k][:, gt, :] if k in PASSES_APART else wide[k][:, 2 * (gt % 4) + gt // 4, :]
             if eng == "v":
-                nc.vector.tensor_scalar(out=wide[k][:, gt, :], in0=src, scalar1=w_scale[:, gt : gt + 1], scalar2=None, op0=ALU.mult)
+                nc.vector.tensor_scalar(out=dst, in0=src, scalar1=w_scale[:, gt : gt + 1], scalar2=None, op0=ALU.mult)
             else:
-                nc.scalar.activation(out=wide[k][:, gt, :], in_=src, func=ACT.Copy, scale=w_scale[:, gt : gt + 1])
+                nc.scalar.activation(out=dst, in_=src, func=ACT.Copy, scale=w_scale[:, gt : gt + 1])
 
         def interleave_pass(k, g, eng):
             if k not in grp:
@@ -150,6 +161,13 @@ def tile_multiheadattentionunit_pa_kernel(tc, attn, Wo_bytes, Wo_scale, bo, quer
                 nc.vector.tensor_copy(out=dst, in_=src)
             else:
                 nc.scalar.copy(out=dst, in_=src)
+
+        def interleave_part(k):
+            grp[k] = grp_pool.tile([P, 8 * HALF], BF16, name="grp", align_bytes=64)
+            nc.vector.tensor_copy(
+                out=grp[k][:].rearrange("p (c i t) -> p c t i", i=4, t=4),
+                in_=wide[k][:].rearrange("p (t g) n -> p t (g n)", g=2).rearrange("p t (c i) -> p c t i", i=4),
+            )
 
         def interleave_cols(k, g, n0, n1):
             if k not in grp:
@@ -252,12 +270,13 @@ def tile_multiheadattentionunit_pa_kernel(tc, attn, Wo_bytes, Wo_scale, bo, quer
 
         def widen_lists(t):
             s_rows, v_rows = [], []
-            for kw in ((t + 1,) if t < DOUBLE_AT else (t + 1, t + 2) if t == DOUBLE_AT else (t + 2,)):
-                if kw < NPART:
+            for kw in range(NPART):
+                if (-1 if kw == 0 else WIDEN_AT.get(kw, max(0, kw - 2))) == t:
                     wide[kw] = wide_pool.tile([P, 8, HALF], BF16, name="wide")
                     nv = NV.get(kw, NV1 if kw < H + 2 else NV2)
-                    s_rows.extend((kw, gt, "s") for gt in range(8 - nv))
-                    v_rows.extend((kw, gt, "v") for gt in range(8 - nv, 8))
+                    order = VFIRST.get(kw, tuple(range(8 - nv, 8)))
+                    v_rows.extend((kw, gt, "v") for gt in order)
+                    s_rows.extend((kw, gt, "s") for gt in range(8) if gt not in order)
             return s_rows, v_rows
 
         def some(rows, n):
@@ -287,8 +306,11 @@ def tile_multiheadattentionunit_pa_kernel(tc, attn, Wo_bytes, Wo_scale, bo, quer
                 product(kp, 0, ps_mx, "mxa")
                 product(kp, 1, ps_mx, "mxb")
             if has_k:
-                interleave_pass(t, 0, "v")
-                interleave_pass(t, 1, "v")
+                if t == 0:
+                    interleave_pass(t, 0, "v")
+                    interleave_pass(t, 1, "v")
+                else:
+                    interleave_part(t)
             some(s_rows, SW[0] if has_p else 3)
             if has_p:
                 empty(kp, 0)
@@ -349,25 +371,17 @@ def tile_multiheadattentionunit_pa_kernel(tc, attn, Wo_bytes, Wo_scale, bo, quer
             flush()
             if kp == H:
                 open_acc(1)
-            if t == NPART - 1:
+            if t in SPLIT:
                 Q = HALF // 2
-                interleave_cols(t, 0, 0, Q)
-                interleave_cols(t, 1, 0, Q)
-                interleave_cols(t, 0, Q, HALF)
-                quant_cols(t, 0, 0, Q)
-                quant_cols(t, 1, 0, Q)
-                interleave_cols(t, 1, Q, HALF)
-                quant_cols(t, 0, Q, HALF)
-                quant_cols(t, 1, Q, HALF)
+                for what, g, q in LASTORD[t] if t in LASTORD else LASTORD[15]:
+                    (interleave_cols if what == "i" else quant_cols)(t, g, Q * q if q < 2 else 0, Q * q + Q if q < 2 else HALF)
             elif has_k:
-                interleave_pass(t, 0, "v")
-                if t not in S_INTER:
-                    interleave_pass(t, 1, "v")
+                interleave_part(t)
                 if t == H - 1:
                     quant_a(2 * t)
             some(v_rows, 1)
-            some(s_rows, 1)
-            if has_k and t < NPART - 1:
+            some(s_rows, S1.get(t, 1))
+            if has_k and t not in SPLIT:
                 quant_w(t)
                 if t == H - 1:
                     quant_a(2 * t + 1)
@@ -383,16 +397,18 @@ def tile_multiheadattentionunit_pa_kernel(tc, attn, Wo_bytes, Wo_scale, bo, quer
                     if kp < NPART - 2 or cc not in MERGE:
                         if cc < 2:
                             if cc == 1:
-                                some(s_rows, 2)
+                                some(s_rows, S2.get(t, 2))
                                 add_up(kp, 0)
                                 add_up(kp, 1)
                         else:
                             pending.append((kp, cc))
             some(v_rows, 8)
             some(s_rows, 8)
-            if t in (NPART - 2, NPART - 1):
-                for j in ((0, 1) if t == NPART - 2 else (2, 3)):
+            if t in SQ:
+                for j in SQ[t]:
                     nc.scalar.activation(out=junk[:], in_=x0[:, j, :], func=ACT.Square, bias=negm[:, 0, j : j + 1], accum_out=rec[:, j, 0, 2:3])
+                if t == max(SQ):
+                    nc.gpsimd.tensor_scalar(out=rec[:, :, 0, 2], in0=rec[:, :, 0, 2], scalar1=1.0, scalar2=D * LN_EPS, op0=ALU.mult, op1=ALU.add)
             loads(t)
 
         nc.tensor.transpose(bo_t[:], bo_rows[:], ident_b[:])
@@ -406,21 +422,17 @@ def tile_multiheadattentionunit_pa_kernel(tc, attn, Wo_bytes, Wo_scale, bo, quer
 
         out_rows = out.rearrange("b (j p) d -> (b j) p d", p=P)
         mv = const.tile([P, NJ, 2], F32, name="mv")
-        ve = const.tile([P, NJ], F32, name="ve")
         rstd = const.tile([P, NJ], F32, name="rstd")
 
         def scalar_sum(j):
-            nc.scalar.activation(out=junk[:], in_=acc[j][:], func=ACT.Identity, accum_out=s_sum[:, 1, j : j + 1])
-            nc.scalar.activation(out=negm[:, 1, j : j + 1], in_=s_sum[:, 1, j : j + 1], func=ACT.Copy, scale=-1.0 / HALF)
-            nc.scalar.activation(out=rec[:, j, 1, 1:2], in_=s_sum[:, 1, j : j + 1], func=ACT.Copy, scale=1.0 / HALF)
+            nc.scalar.activation(out=junk[:], in_=acc[j][:], func=ACT.Identity, scale=1.0 / HALF, accum_out=rec[:, j, 1, 1:2])
 
         def scalar_squares(j):
-            nc.scalar.activation(out=junk[:], in_=acc[j][:], func=ACT.Square, bias=negm[:, 1, j : j + 1], accum_out=rec[:, j, 1, 2:3])
+            nc.scalar.activation(out=junk[:], in_=acc[j][:], func=ACT.Square, scale=-1.0, bias=rec[:, j, 1, 1:2], accum_out=rec[:, j, 1, 2:3])
 
         def aggregate(j, n):
             nc.vector.bn_aggr(out=mv[:, j, :], in_=rec[:, j, 0:n, 0:3])
-            nc.gpsimd.tensor_scalar(out=ve[:, j : j + 1], in0=mv[:, j, 1:2], scalar1=1.0, scalar2=LN_EPS, op0=ALU.mult, op1=ALU.add)
-            nc.gpsimd.tensor_tensor(out=rstd[:, j : j + 1], in0=ve[:, j : j + 1], in1=minus_half[:, 0:1], op=ALU.pow)
+            nc.gpsimd.tensor_tensor(out=rstd[:, j : j + 1], in0=mv[:, j, 1:2], in1=minus_half[:, 0:1], op=ALU.pow)
 
         LAST = NJ - 1
         nmr = const.tile([P, 1], F32, name="nmr")

@@ -24,11 +24,11 @@ HALF = 512
 NPART = 2 * H
 WA = 2
 
-NV = {0: 5, 1: 5, 2: 5, 11: 6, 13: 4, 14: 3, 15: 3}
+NV = {0: 4, 1: 5, 2: 5, 9: 6, 11: 6, 13: 4, 14: 3, 15: 3}
 NV1, NV2 = 5, 4
 PASSES_APART = (0, NPART - 1)
 SPLIT = (NPART - 1,)
-VFIRST = {0: (0, 1, 2, 3, 4), 15: (0, 1, 2, 3)}
+VFIRST = {0: (0, 1, 2, 4), 15: (0, 1, 2, 3)}
 S1 = {}
 S2 = {}
 LASTORD = {15: (("i", 0, 0), ("i", 0, 1), ("i", 1, 0), ("q", 0, 0), ("q", 1, 0), ("i", 1, 1), ("q", 0, 1), ("q", 1, 1))}

from contextlib import ExitStack

import concourse.mybir as mybir
from concourse.masks import make_identity

B, H, S, DV, D = 2, 8, 256, 1024, 1024
LN_EPS = 1e-3
FLOPS = 2 * B * H * S * DV * D

F32 = mybir.dt.float32
BF16 = mybir.dt.bfloat16
U32 = mybir.dt.uint32
U8 = mybir.dt.uint8
FP8 = mybir.dt.float8_e4m3fn
FP8X4 = mybir.dt.float8_e4m3fn_x4
ACT = mybir.ActivationFunctionType
ALU = mybir.AluOpType
AX = mybir.AxisListType

P = 128
NTOK = B * S
NJ = NTOK // P
HALF = 512
NPART = 2 * H
WA = 2

NV = {0: 4, 1: 5, 2: 5, 9: 6, 11: 6, 13: 4, 14: 3, 15: 3}
NV1, NV2 = 5, 4
PASSES_APART = (0, NPART - 1)
SPLIT = (NPART - 1,)
VFIRST = {0: (0, 1, 2, 4), 15: (0, 1, 2, 3)}
S1 = {}
S2 = {}
LASTORD = {15: (("i", 0, 0), ("i", 0, 1), ("i", 1, 0), ("q", 0, 0), ("q", 1, 0), ("i", 1, 1), ("q", 0, 1), ("q", 1, 1))}

WIDEN_AT = {15: 14}
SQ = {15: (0, 1), 16: (2, 3)}

SW = (1, 1, 1)
VW = (2,)
STORE_AFTER = 0
DOUBLE_AT = 0
MERGE = (0, 1, 2, 3)
S_INTER = ()
V_EMPTY = {15: (1, 3)}


def tile_multiheadattentionunit_pa_kernel(tc, attn, Wo_bytes, Wo_scale, bo, query_inputs, gamma, beta, out):
    nc = tc.nc
    with ExitStack() as ctx:
        const = ctx.enter_context(tc.tile_pool(name="const", bufs=1))
        wb_pool = ctx.enter_context(tc.tile_pool(name="wb", bufs=5))
        wide_pool = ctx.enter_context(tc.tile_pool(name="wide", bufs=3))
        grp_pool = ctx.enter_context(tc.tile_pool(name="grp", bufs=2))
        wc_pool = ctx.enter_context(tc.tile_pool(name="wc", bufs=3))
        at_pool = ctx.enter_context(tc.tile_pool(name="at", bufs=6))
        ag_pool = ctx.enter_context(tc.tile_pool(name="ag", bufs=3))
        r_pool = ctx.enter_context(tc.tile_pool(name="r", bufs=8))
        cen_pool = ctx.enter_context(tc.tile_pool(name="cen", bufs=2))
        res_pool = ctx.enter_context(tc.tile_pool(name="res", bufs=3))
        ps_acc = ctx.enter_context(tc.psum_pool(name="ps_acc", bufs=1))
        ps_mx = ctx.enter_context(tc.psum_pool(name="ps_mx", bufs=1))
        ps_tr = ctx.enter_context(tc.psum_pool(name="ps_tr", bufs=2))
        ctx.enter_context(tc.manual_schedule())

        wb, wide, grp, wc, ws, at, ag, ac, asc = {}, {}, {}, {}, {}, {}, {}, {}, {}

        def load_w(k):
            s, h = divmod(k, H)
            wb[k] = wb_pool.tile([P, 8, HALF], U8, name="wbytes")
            for g in range(2):
                nc.sync.dma_start(
                    out=wb[k][:, 4 * g : 4 * g + 4, :],
                    in_=Wo_bytes[h, 512 * g : 512 * (g + 1), HALF * s : HALF * (s + 1)].rearrange("(p t) n -> p t n", t=4),
                )

        def load_a(h):
            for b in range(B):
                at[h, b] = at_pool.tile([P, 2, DV], BF16, name="araw")
                nc.sync.dma_start(out=at[h, b][:], in_=attn[b, h].rearrange("(j p) k -> p j k", p=P))

        w_scale = const.tile([P, 8], F32, name="w_scale")
        nc.sync.dma_start(
            out=w_scale[:].rearrange("p (g t) -> p g t", g=2),
            in_=Wo_scale.rearrange("o (g p t) x -> p (o g) (t x)", g=2, p=P, t=4),
        )
        load_w(0)
        bo_rows = const.tile([P, P], BF16, name="bo_rows")
        nc.vector.memset(bo_rows[:], 0.0)
        nc.sync.dma_start(out=bo_rows[0 : 8 * H, :], in_=bo.rearrange("h (c p) -> (h c) p", p=P))
        nc.sync.dma_start(out=bo_rows[8 * H : 8 * H + 8, :], in_=gamma.rearrange("(c p) -> c p", p=P))
        nc.sync.dma_start(out=bo_rows[8 * H + 8 : 8 * H + 16, :], in_=beta.rearrange("(c p) -> c p", p=P))
        q_sb = const.tile([P, 2, NJ, HALF], BF16, name="q_sb")

        def load_q(s):
            nc.sync.dma_start(out=q_sb[:, s, :, :], in_=query_inputs[:, :, HALF * s : HALF * (s + 1)].rearrange("b (j p) d -> p (b j) d", p=P))

        load_a(0)
        load_w(1)
        load_w(2)
        load_a(1)
        load_q(0)
        load_w(3)
        load_a(2)
        load_w(4)

        ident_f = const.tile([P, P], F32, name="ident_f")
        make_identity(nc, ident_f[:])
        ident_b = const.tile([P, P], BF16, name="ident_b")
        make_identity(nc, ident_b[:])

        one = const.tile([P, 1], F32, name="one")
        nc.vector.memset(one[:], 1.0)
        one2 = const.tile([P, 1], F32, name="one2")
        nc.scalar.activation(out=one2[:], in_=one[:], func=ACT.Square)

        minus_half = const.tile([P, 4], F32, name="minus_half")
        nc.gpsimd.memset(minus_half[:], -0.5)

        bcol = const.tile([P, 8 * H + 16], F32, name="bcol")
        negb = const.tile([P, 8 * H], F32, name="negb")
        first_row = const.tile([P, P], BF16, name="first_row")
        nc.vector.memset(first_row[:], 0.0)
        nc.vector.memset(first_row[0:1, :], 1.0)
        b_last = const.tile([P, HALF], BF16, name="b_last")
        nc.vector.memset(b_last[:], 0.0)
        x0 = const.tile([P, NJ, HALF], F32, name="x0")
        gam = const.tile([P, D], BF16, name="gam")
        bet = const.tile([P, D], BF16, name="bet")
        acc = [ps_acc.tile([P, HALF], F32, name="acc%d" % j) for j in range(NJ)]
        for h in range(H):
            ac[h] = const.tile([P, 2, NTOK], U32, name="acodes%d" % h, align_bytes=64)
            asc[h] = const.tile([P, 2, NTOK], U8, name="ascales%d" % h, align_bytes=64)

        bo_t = ps_mx.tile([P, P], BF16, name="bo_t", tag="mxa")

        def prepare_bias():
            nc.vector.tensor_copy(out=bcol[:], in_=bo_t[:, 0 : 8 * H + 16])
            nc.vector.tensor_scalar(out=negb[:], in0=bcol[:, 0 : 8 * H], scalar1=-1.0, scalar2=None, op0=ALU.mult)

        def open_acc(s):
            for j in range(NJ):
                nc.tensor.matmul(out=acc[j][:], lhsT=ident_b[:], rhs=q_sb[:, s, j, :], start=True, stop=False)
                if s == 1:
                    nc.tensor.matmul(out=acc[j][:], lhsT=first_row[:], rhs=b_last[:], start=False, stop=False)

        def widen(k, gt, eng):
            src = wb[k][:, gt, :].bitcast(FP8)
            dst = wide[k][:, gt, :] if k in PASSES_APART else wide[k][:, 2 * (gt % 4) + gt // 4, :]
            if eng == "v":
                nc.vector.tensor_scalar(out=dst, in0=src, scalar1=w_scale[:, gt : gt + 1], scalar2=None, op0=ALU.mult)
            else:
                nc.scalar.activation(out=dst, in_=src, func=ACT.Copy, scale=w_scale[:, gt : gt + 1])

        def interleave_pass(k, g, eng):
            if k not in grp:
                grp[k] = grp_pool.tile([P, 8 * HALF], BF16, name="grp", align_bytes=64)
            dst = grp[k][:, 4 * HALF * g : 4 * HALF * (g + 1)].rearrange("p (c i t) -> p c t i", i=4, t=4)
            src = wide[k][:, 4 * g : 4 * g + 4, :].rearrange("p t (c i) -> p c t i", i=4)
            if eng == "v":
                nc.vector.tensor_copy(out=dst, in_=src)
            else:
                nc.scalar.copy(out=dst, in_=src)

        def interleave_part(k):
            grp[k] = grp_pool.tile([P, 8 * HALF], BF16, name="grp", align_bytes=64)
            nc.vector.tensor_copy(
                out=grp[k][:].rearrange("p (c i t) -> p c t i", i=4, t=4),
                in_=wide[k][:].rearrange("p (t g) n -> p t (g n)", g=2).rearrange("p t (c i) -> p c t i", i=4),
            )

        def interleave_cols(k, g, n0, n1):
            if k not in grp:
                grp[k] = grp_pool.tile([P, 8 * HALF], BF16, name="grp", align_bytes=64)
            dst = grp[k][:, 4 * (HALF * g + n0) : 4 * (HALF * g + n1)].rearrange("p (c i t) -> p c t i", i=4, t=4)
            src = wide[k][:, 4 * g : 4 * g + 4, n0:n1].rearrange("p t (c i) -> p c t i", i=4)
            nc.vector.tensor_copy(out=dst, in_=src)

        def quant_cols(k, g, n0, n1):
            if k not in wc:
                wc[k] = wc_pool.tile([P, 2 * HALF], U32, name="wcodes", align_bytes=64)
                ws[k] = wc_pool.tile([P, 2 * HALF], U8, name="wscales", align_bytes=64)
            cols = slice(HALF * g + n0, HALF * g + n1)
            nc.vector.quantize_mx(out=wc[k][:, cols].bitcast(FP8X4), scales=ws[k][:, cols], in_=grp[k][:, 4 * (HALF * g + n0) : 4 * (HALF * g + n1)])

        def quant_w(k):
            wc[k] = wc_pool.tile([P, 2 * HALF], U32, name="wcodes", align_bytes=64)
            ws[k] = wc_pool.tile([P, 2 * HALF], U8, name="wscales", align_bytes=64)
            nc.vector.quantize_mx(out=wc[k][:].bitcast(FP8X4), scales=ws[k][:], in_=grp[k][:])

        xt = {}

        def a_transpose(a, b):
            h, g = divmod(a, 2)
            xt[a, b] = ps_tr.tile([P, 2, 2 * P], F32, name="xt", tag="tr")
            for j in range(2):
                words = at[h, b][:, j, :].bitcast(F32)
                for u in range(2):
                    nc.tensor.transpose(xt[a, b][:, u, P * j : P * (j + 1)], words[:, 256 * g + u : 256 * (g + 1) : 2], ident_f[:])

        def a_evac(a, b, eng="s"):
            if b == 0:
                ag[a] = ag_pool.tile([P, 4 * NTOK], BF16, name="agrp", align_bytes=64)
            dst = ag[a][:, 1024 * b : 1024 * (b + 1)].bitcast(F32).rearrange("p (r u) -> p r u", u=2)
            src = xt[a, b][:].rearrange("p u r -> p r u")
            if eng == "s":
                nc.scalar.copy(out=dst, in_=src)
            else:
                nc.vector.tensor_copy(out=dst, in_=src)

        def quant_a(a):
            h, g = divmod(a, 2)
            nc.vector.quantize_mx(out=ac[h][:, g, :].bitcast(FP8X4), scales=asc[h][:, g, :], in_=ag[a][:])

        mx = {}
        r = {}

        def product(k, cc, pool, tag):
            h = k % H
            mx[k, cc] = pool.tile([P, NTOK], F32, name="mx", tag=tag)
            for g in range(2):
                cols = slice(HALF * g + P * cc, HALF * g + P * (cc + 1))
                nc.tensor.matmul_mx(
                    out=mx[k, cc][:],
                    lhsT=wc[k][:, cols].bitcast(FP8X4),
                    lhsT_scale=ws[k][:, cols],
                    rhs=ac[h][:, g, :].bitcast(FP8X4),
                    rhs_scale=asc[h][:, g, :],
                    start=(g == 0),
                    stop=(g == 1),
                )

        def empty(k, cc, eng="s"):
            s, h = divmod(k, H)
            col = 8 * h + 4 * s + cc
            r[k, cc] = r_pool.tile([P, NTOK], F32, name="relu")
            if eng == "s":
                nc.scalar.activation(out=r[k, cc][:], in_=mx[k, cc][:], func=ACT.Relu, bias=bcol[:, col : col + 1])
            else:
                nc.vector.tensor_scalar(out=r[k, cc][:], in0=mx[k, cc][:], scalar1=bcol[:, col : col + 1], scalar2=0.0,
                                        op0=ALU.add, op1=ALU.max)

        def empty_onto(k, cc, k_before):
            s, h = divmod(k, H)
            col = 8 * h + 4 * s + cc
            r[k, cc] = r_pool.tile([P, NTOK], F32, name="relu")
            nc.vector.scalar_tensor_tensor(out=r[k, cc][:], in0=mx[k, cc][:], scalar=negb[:, col : col + 1], in1=r[k_before, cc][:],
                                           op0=ALU.max, op1=ALU.add)

        def add_up(k, cc):
            last = k % H == H - 1 and cc == 3
            for j in ((3, 0, 1, 2) if last else range(NJ)):
                nc.tensor.matmul(out=acc[j][:, P * cc : P * (cc + 1)], lhsT=r[k, cc][:, P * j : P * (j + 1)], rhs=ident_f[:],
                                 is_transpose=True, start=False, stop=last)

        rec = const.tile([P, NJ, 3, 8], F32, name="rec")
        nc.gpsimd.memset(rec[:], float(HALF))
        s_sum = const.tile([P, 2, NJ], F32, name="s_sum")
        negm = const.tile([P, 2, NJ], F32, name="negm")
        junk = const.tile([P, HALF], F32, name="junk")
        pending = []

        def which(k, cc):
            return "v" if cc in V_EMPTY.get(k, ()) else "s"

        def flush():
            for item in pending:
                add_up(*item)
            pending.clear()

        def widen_lists(t):
            s_rows, v_rows = [], []
            for kw in range(NPART):
                if (-1 if kw == 0 else WIDEN_AT.get(kw, max(0, kw - 2))) == t:
                    wide[kw] = wide_pool.tile([P, 8, HALF], BF16, name="wide")
                    nv = NV.get(kw, NV1 if kw < H + 2 else NV2)
                    order = VFIRST.get(kw, tuple(range(8 - nv, 8)))
                    v_rows.extend((kw, gt, "v") for gt in order)
                    s_rows.extend((kw, gt, "s") for gt in range(8) if gt not in order)
            return s_rows, v_rows

        def some(rows, n):
            for item in rows[0:n]:
                widen(*item)
                rows.remove(item)

        def loads(t):
            if t >= 0 and t + 5 < NPART:
                load_w(t + 5)
            if t == 4:
                load_q(1)
                for cc in MERGE:
                    nc.sync.dma_start(out=b_last[0:1, P * cc : P * (cc + 1)], in_=bo[H - 1 : H, HALF + P * cc : HALF + P * (cc + 1)])
            if t >= 0 and t + 3 < H:
                load_a(t + 3)
            if t == 8:
                nc.sync.dma_start(out=gam[:], in_=gamma.partition_broadcast(P))
                nc.sync.dma_start(out=bet[:], in_=beta.partition_broadcast(P))

        def tick1(t):
            kp, ha = t - 1, t + 1
            has_p, has_k = kp >= 0, t >= 0
            s_rows, v_rows = widen_lists(t)
            flush()
            if has_p:
                product(kp, 0, ps_mx, "mxa")
                product(kp, 1, ps_mx, "mxb")
            if has_k:
                if t == 0:
                    interleave_pass(t, 0, "v")
                    interleave_pass(t, 1, "v")
                else:
                    interleave_part(t)
            some(s_rows, SW[0] if has_p else 3)
            if has_p:
                empty(kp, 0)
                empty(kp, 1)
            if ha >= 0:
                a_transpose(2 * ha, 0)
                a_transpose(2 * ha, 1)
            if kp == 0:
                open_acc(0)
            if has_p:
                add_up(kp, 0)
                add_up(kp, 1)
                product(kp, 2, ps_mx, "mxa")
                product(kp, 3, ps_mx, "mxb")
            some(s_rows, SW[1])
            if t == DOUBLE_AT:
                some(v_rows, 5)
            if has_k:
                quant_a(2 * t)
            some(v_rows, VW[0])
            if ha >= 0:
                a_evac(2 * ha, 0)
                a_evac(2 * ha, 1)
            some(s_rows, SW[2])
            if has_k:
                quant_w(t)
            if has_p:
                empty(kp, 2)
                empty(kp, 3)
                pending.append((kp, 2))
                pending.append((kp, 3))
            if ha >= 0:
                a_transpose(2 * ha + 1, 0)
                a_transpose(2 * ha + 1, 1)
            some(s_rows, 8)
            if has_k:
                quant_a(2 * t + 1)
            some(v_rows, 8)
            if ha >= 0:
                a_evac(2 * ha + 1, 0)
                a_evac(2 * ha + 1, 1)
            loads(t)

        BANKS = ((ps_mx, "mxa"), (ps_mx, "mxb"), (ps_tr, "tr"), (ps_tr, "tr"))

        def tick2(t):
            kp = t - 1
            has_k = t < NPART
            s_rows, v_rows = widen_lists(t)
            if kp == H:
                flush()
                for j in range(NJ):
                    nc.scalar.activation(out=x0[:, j, :], in_=acc[j][:], func=ACT.Identity, accum_out=s_sum[:, 0, j : j + 1])
                nc.gpsimd.tensor_scalar(out=rec[:, :, 0, 1], in0=s_sum[:, 0, :], scalar1=1.0 / HALF, scalar2=0.0, op0=ALU.mult, op1=ALU.add)
                nc.gpsimd.tensor_scalar(out=negm[:, 0, :], in0=s_sum[:, 0, :], scalar1=-1.0 / HALF, scalar2=0.0, op0=ALU.mult, op1=ALU.add)
            for cc in range(4):
                product(kp, cc, *BANKS[cc])
            flush()
            if kp == H:
                open_acc(1)
            if t in SPLIT:
                Q = HALF // 2
                for what, g, q in LASTORD[t] if t in LASTORD else LASTORD[15]:
                    (interleave_cols if what == "i" else quant_cols)(t, g, Q * q if q < 2 else 0, Q * q + Q if q < 2 else HALF)
            elif has_k:
                interleave_part(t)
                if t == H - 1:
                    quant_a(2 * t)
            some(v_rows, 1)
            some(s_rows, S1.get(t, 1))
            if has_k and t not in SPLIT:
                quant_w(t)
                if t == H - 1:
                    quant_a(2 * t + 1)
            for cc in range(4):
                if kp == NPART - 1:
                    if cc in MERGE:
                        empty_onto(kp, cc, kp - 1)
                    else:
                        empty(kp, cc)
                    add_up(kp, cc)
                else:
                    empty(kp, cc)
                    if kp < NPART - 2 or cc not in MERGE:
                        if cc < 2:
                            if cc == 1:
                                some(s_rows, S2.get(t, 2))
                                add_up(kp, 0)
                                add_up(kp, 1)
                        else:
                            pending.append((kp, cc))
            some(v_rows, 8)
            some(s_rows, 8)
            if t in SQ:
                for j in SQ[t]:
                    nc.scalar.activation(out=junk[:], in_=x0[:, j, :], func=ACT.Square, bias=negm[:, 0, j : j + 1], accum_out=rec[:, j, 0, 2:3])
                if t == max(SQ):
                    nc.gpsimd.tensor_scalar(out=rec[:, :, 0, 2], in0=rec[:, :, 0, 2], scalar1=1.0, scalar2=D * LN_EPS, op0=ALU.mult, op1=ALU.add)
            loads(t)

        nc.tensor.transpose(bo_t[:], bo_rows[:], ident_b[:])
        tick1(-1)
        prepare_bias()
        for t in range(0, H - 1):
            tick1(t)
        for t in range(H - 1, NPART + 1):
            tick2(t)
        flush()

        out_rows = out.rearrange("b (j p) d -> (b j) p d", p=P)
        mv = const.tile([P, NJ, 2], F32, name="mv")
        rstd = const.tile([P, NJ], F32, name="rstd")

        def scalar_sum(j):
            nc.scalar.activation(out=junk[:], in_=acc[j][:], func=ACT.Identity, scale=1.0 / HALF, accum_out=rec[:, j, 1, 1:2])

        def scalar_squares(j):
            nc.scalar.activation(out=junk[:], in_=acc[j][:], func=ACT.Square, scale=-1.0, bias=rec[:, j, 1, 1:2], accum_out=rec[:, j, 1, 2:3])

        def aggregate(j, n):
            nc.vector.bn_aggr(out=mv[:, j, :], in_=rec[:, j, 0:n, 0:3])
            nc.gpsimd.tensor_tensor(out=rstd[:, j : j + 1], in0=mv[:, j, 1:2], in1=minus_half[:, 0:1], op=ALU.pow)

        LAST = NJ - 1
        nmr = const.tile([P, 1], F32, name="nmr")
        nc.vector.bn_stats(out=rec[:, LAST, 1:3, 0:3], in_=acc[LAST][:])
        scalar_sum(2)
        aggregate(LAST, 3)
        nc.gpsimd.tensor_scalar(out=nmr[:], in0=mv[:, LAST, 0:1], scalar1=rstd[:, LAST : LAST + 1], scalar2=-1.0, op0=ALU.mult, op1=ALU.mult)
        nc.vector.bn_stats(out=rec[:, 0, 1:3, 0:3], in_=acc[0][:])
        nc.vector.bn_stats(out=rec[:, 1, 1:3, 0:3], in_=acc[1][:])
        scalar_squares(2)
        aggregate(0, 3)

        norm = const.tile([P, D], F32, name="norm")
        turned = const.tile([P, 8, P], F32, name="turned")
        res_last = const.tile([P, D], F32, name="res_last")
        for i in range(2):
            nc.scalar.activation(out=norm[:, HALF * i : HALF * (i + 1)], in_=(x0[:, LAST, :] if i == 0 else acc[LAST][:]), func=ACT.Identity,
                                 scale=rstd[:, LAST : LAST + 1], bias=nmr[:])
        for i in range(2):
            there = ps_mx.tile([P, 4, P], F32, name="there", tag=("mxa", "mxb")[i])
            for c in range(4):
                nc.tensor.transpose(there[:, c, :], norm[:, HALF * i + P * c : HALF * i + P * (c + 1)], ident_f[:])
            for c in range(4):
                col = 8 * H + 4 * i + c
                nc.scalar.activation(out=turned[:, 4 * i + c, :], in_=there[:, c, :], func=ACT.Identity, scale=bcol[:, col : col + 1],
                                     bias=bcol[:, col + 8 : col + 9])
        for i in range(2):
            back = ps_tr.tile([P, 4, P], F32, name="back", tag="tr")
            for c in range(4):
                nc.tensor.transpose(back[:, c, :], turned[:, 4 * i + c, :], ident_f[:])
            nc.scalar.copy(out=res_last[:, HALF * i : HALF * (i + 1)], in_=back[:].rearrange("p c t -> p (c t)"))
            nc.scalar.dma_start(out=out_rows[LAST][:, HALF * i : HALF * (i + 1)], in_=res_last[:, HALF * i : HALF * (i + 1)])

        cen = {}

        def centre(j, i):
            if i == 0:
                cen[j] = cen_pool.tile([P, D], F32, name="cen")
            src = x0[:, j, :] if i == 0 else acc[j][:]
            c0 = HALF * i
            nc.vector.scalar_tensor_tensor(out=cen[j][:, c0 : c0 + HALF], in0=src, scalar=mv[:, j, 0:1], in1=gam[:, c0 : c0 + HALF],
                                           op0=ALU.subtract, op1=ALU.mult)

        def finish(j):
            scale = rstd[:, j : j + 1]
            res = res_pool.tile([P, D], F32, name="res")
            pieces = ((0, D),) if j < NJ - 2 else ((0, HALF), (HALF, D))
            for c0, c1 in pieces:
                nc.vector.scalar_tensor_tensor(out=res[:, c0:c1], in0=cen[j][:, c0:c1], scalar=scale, in1=bet[:, c0:c1],
                                               op0=ALU.mult, op1=ALU.add)
                nc.sync.dma_start(out=out_rows[j][:, c0:c1], in_=res[:, c0:c1])

        centre(0, 0)
        for j in range(LAST):
            if j + 1 < LAST:
                aggregate(j + 1, 3 if j + 1 < 2 else 2)
            centre(j, 1)
            if j + 1 < LAST:
                centre(j + 1, 0)
            finish(j)
